import numpy as np
import ml_dtypes


def mxq(x, axis, fmt="e4m3"):
    dtype, down = {"e4m3": (ml_dtypes.float8_e4m3fn, 7), "e5m2": (ml_dtypes.float8_e5m2, 14)}[fmt]
    v = np.moveaxis(np.asarray(x, np.float32).astype(ml_dtypes.bfloat16).astype(np.float64), axis, -1)
    blocks = v.reshape(v.shape[:-1] + (-1, 32))
    amax = np.abs(blocks).max(-1, keepdims=True)
    byte = np.maximum(np.where(amax > 0, np.frexp(amax)[1] - 1 + 127, 0) - down, 1)
    scale = np.exp2(byte - 127.0)
    codes = (blocks / scale).astype(np.float32).astype(dtype).astype(np.float64)
    return np.moveaxis((codes * scale).reshape(v.shape), -1, axis)


WIDE = False


def mx_kscale(k):
    if not WIDE:
        return np.ones(k)
    levels = np.array([10, -10, 5, -5, 0])
    if k % 512:
        return np.exp2(np.random.permutation(np.resize(levels, k // 32))).repeat(32)
    a = np.empty((k // 512, 16))
    for p in range(k // 512):
        a[p, :8] = np.random.permutation(np.resize(levels, 8))
        for g in range(8):
            far = levels[np.abs(levels - a[p, g]) >= 10]
            a[p, g + 8] = far[np.random.randint(len(far))]
    return np.exp2(a.ravel()).repeat(32)


BF16 = ml_dtypes.bfloat16


def bf(x):
    return np.asarray(x, np.float32).astype(BF16)


def f64(x):
    return np.asarray(x).astype(np.float64)


B, DIN, DOUT = 16384, 512, 128

MIN_NORM = 1e-15
PROJ_EPS = 1e-3
W_MUL = 0.1
B_MUL = 0.1
C = 1.0


def artanh(x):
    x = np.clip(x, -1.0 + 1e-5, 1.0 - 1e-5)
    return 0.5 * (np.log1p(x) - np.log1p(-x))


def mobius_matvec(w, x, c):
    sqrt_c = c ** 0.5
    x_norm = np.maximum(np.linalg.norm(x, axis=-1, keepdims=True), MIN_NORM)
    mx = mxq(x, 1, "e4m3") @ mxq(w, 1, "e4m3").T
    mx_norm = np.maximum(np.linalg.norm(mx, axis=-1, keepdims=True), MIN_NORM)
    res = np.tanh(mx_norm / x_norm * artanh(sqrt_c * x_norm)) * mx / (mx_norm * sqrt_c)
    zero_row = np.all(mx == 0, axis=-1, keepdims=True)
    return np.where(zero_row, 0.0, res)


def expmap0(u, c):
    sqrt_c = c ** 0.5
    u_norm = np.maximum(np.linalg.norm(u, axis=-1, keepdims=True), MIN_NORM)
    return np.tanh(sqrt_c * u_norm) * u / (sqrt_c * u_norm)


def mobius_add(x, y, c):
    x2 = np.sum(x * x, axis=-1, keepdims=True)
    y2 = np.sum(y * y, axis=-1, keepdims=True)
    xy = np.sum(x * y, axis=-1, keepdims=True)
    num = (1 + 2 * c * xy + c * y2) * x + (1 - c * x2) * y
    denom = 1 + 2 * c * xy + c * c * x2 * y2
    return num / np.maximum(denom, MIN_NORM)


def project(x, c):
    sqrt_c = c ** 0.5
    norm = np.maximum(np.linalg.norm(x, axis=-1, keepdims=True), MIN_NORM)
    maxnorm = (1.0 - PROJ_EPS) / sqrt_c
    return np.where(norm > maxnorm, x / norm * maxnorm, x)


def setup_inputs():
    s = mx_kscale(DIN)
    g = np.exp2(np.ceil(np.log2(np.sqrt(np.mean(s * s)))))
    return {"x": bf(np.random.standard_normal((B, DIN)) * 0.7 / np.sqrt(DIN) * s / g),
            "weight": bf(np.random.standard_normal((DOUT, DIN)) * 10.0 / np.sqrt(DOUT) * g / s),
            "bias": bf(np.random.standard_normal(DOUT) * 3.0 / np.sqrt(DOUT))}


def reference(x, weight, bias):
    c = C
    w_lr = f64(weight) * W_MUL
    mv = mobius_matvec(w_lr, f64(x), c)
    b = expmap0(f64(bias) * B_MUL, c)
    out = project(mobius_add(mv, b[None, :], 1.0), c)
    return np.where(out >= 0, out, 0.2 * out)

@@ -1,0 +1,447 @@
+from contextlib import ExitStack
+
+import concourse.mybir as mybir
+from concourse.masks import make_identity
+
+FLOPS = 2 * 16384 * 512 * 128
+
+F32 = mybir.dt.float32
+BF16 = mybir.dt.bfloat16
+U32 = mybir.dt.uint32
+U8 = mybir.dt.uint8
+FP8X4 = mybir.dt.float8_e4m3fn_x4
+ALU = mybir.AluOpType
+ACT = mybir.ActivationFunctionType
+
+P = 128
+K = 512
+DOUT = 128
+NT = 128
+CH = 4
+NCH = NT // CH
+GROUPS = (32, 32, 32, 16, 8, 8)
+LOOKAHEAD = 4
+
+
+def tile_hypequalizedlinear_t_kernel(tc, x, weight, bias, out):
+    nc = tc.nc
+    xv = x.rearrange("(p t) k -> p t k", t=NT)
+    ov = out.rearrange("(p t) o -> p t o", t=NT)
+    with ExitStack() as ctx:
+        const = ctx.enter_context(tc.tile_pool(name="const", bufs=1))
+        xpool = ctx.enter_context(tc.tile_pool(name="xpool", bufs=6))
+        gpool = ctx.enter_context(tc.tile_pool(name="gpool", bufs=3))
+        bpool = ctx.enter_context(tc.tile_pool(name="bpool", bufs=3))
+        ypool = ctx.enter_context(tc.tile_pool(name="ypool", bufs=4))
+        ps_xt = ctx.enter_context(tc.psum_pool(name="ps_xt", bufs=2))
+        ps_ms = ctx.enter_context(tc.psum_pool(name="ps_ms", bufs=2))
+        ps_mv = ctx.enter_context(tc.psum_pool(name="ps_mv", bufs=2))
+        ps_m2 = ctx.enter_context(tc.psum_pool(name="ps_m2", bufs=2))
+
+        ctx.enter_context(tc.manual_schedule())
+        v = nc.vector
+        sc = nc.scalar
+
+        def col(name):
+            return const.tile([P, 1], F32, name=name)
+
+        def wide(name, n=1):
+            if n == 1:
+                return const.tile([P, NT], F32, name=name)
+            return const.tile([P, n, NT], F32, name=name)
+
+        ident = const.tile([P, P], F32, name="ident")
+        half = col("half")
+        w_raw = const.tile([P, K], BF16, name="w_raw")
+        bias_bc = const.tile([P, DOUT], BF16, name="bias_bc")
+        junk_c = [const.tile([P, K], BF16, name="junk_c%d" % i) for i in range(4)]
+        junk_d = [const.tile([P, DOUT], F32, name="junk_d%d" % i) for i in range(4)]
+        junk_e = [const.tile([P, DOUT], F32, name="junk_e%d" % i) for i in range(4)]
+        w_grouped = const.tile([P, K], BF16, name="w_grouped", align_bytes=64)
+        w_codes = const.tile([P, DOUT], U32, name="w_codes", align_bytes=64)
+        w_scales = const.tile([P, DOUT], U8, name="w_scales", align_bytes=64)
+        u_f = const.tile([P, DOUT], F32, name="u_f")
+        b_pos = const.tile([P, DOUT], F32, name="b_pos")
+        b_neg = const.tile([P, DOUT], F32, name="b_neg")
+        un2 = col("un2")
+        un2c = col("un2c")
+        un = col("un")
+        th = col("th")
+        run = col("run")
+        kk = col("kk")
+        y2 = col("y2")
+        ym1 = col("ym1")
+        codes = const.tile([P, NT * P], U32, name="codes", align_bytes=64)
+        scales = const.tile([P, NT * P], U8, name="scales", align_bytes=64)
+        s2 = wide("s2", 2)
+        pb = wide("pb")
+        al = wide("al")
+        nbe = wide("nbe")
+        c_s2c = wide("c_s2c", 2)
+        c_nrm = wide("c_nrm", 2)
+        c_rnrm = wide("c_rnrm", 2)
+        c_nv = wide("c_nv")
+        c_dn = wide("c_dn")
+        c_rdn = wide("c_rdn")
+        c_base = wide("c_base")
+        c_r = wide("c_r")
+        c_e = wide("c_e")
+        c_e1 = wide("c_e1")
+        c_re = wide("c_re")
+        c_t = wide("c_t")
+        c_s = wide("c_s")
+        c_x2 = wide("c_x2")
+        c_xy = wide("c_xy")
+        c_c1 = wide("c_c1")
+        c_den = wide("c_den")
+        c_denc = wide("c_denc")
+        c_rden = wide("c_rden")
+        c_num = wide("c_num")
+        c_nn2 = wide("c_nn2")
+        c_nn2c = wide("c_nn2c")
+        c_nn = wide("c_nn")
+        c_rnn = wide("c_rnn")
+        c_f = wide("c_f")
+        c_rf = wide("c_rf")
+        c_as = wide("c_as")
+
+        xs_of = {}
+        xt_of = {}
+        g_of = {}
+        ms_of = {}
+        mv_of = {}
+        m2_of = {}
+        t1_of = {}
+        y_of = {}
+
+        def ts(o, i, s1, s2_, o0, o1=None):
+            if o1 is None:
+                return lambda: v.tensor_scalar(out=o, in0=i, scalar1=s1, scalar2=None, op0=o0)
+            return lambda: v.tensor_scalar(out=o, in0=i, scalar1=s1, scalar2=s2_, op0=o0, op1=o1)
+
+        def tt(o, i0, i1, op):
+            return lambda: v.tensor_tensor(out=o, in0=i0, in1=i1, op=op)
+
+        def stt(o, i0, s, i1, o0, o1, acc=None):
+            return lambda: v.scalar_tensor_tensor(out=o, in0=i0, scalar=s, in1=i1, op0=o0, op1=o1, accum_out=acc)
+
+        def rcp(o, i):
+            return lambda: v.reciprocal(out=o, in_=i)
+
+        def act(o, i, func, acc=None):
+            return lambda: sc.activation(out=o, in_=i, func=func, accum_out=acc)
+
+        def scaled(o, i, s):
+            return lambda: sc.activation(out=o, in_=i, func=ACT.Copy, scale=s)
+
+        def power(o, i0, i1):
+            return lambda: nc.gpsimd.tensor_tensor(out=o, in0=i0, in1=i1, op=ALU.pow)
+
+        def weave(bulk, extra, skip):
+            i = 0
+            for n, f in enumerate(bulk):
+                f()
+                if n >= skip and n % 2 == 0 and i < len(extra):
+                    extra[i]()
+                    i += 1
+            for f in extra[i:]:
+                f()
+
+        def mx(dst, t):
+            nc.tensor.matmul_mx(
+                out=dst,
+                lhsT=codes[:, t * P : (t + 1) * P].bitcast(FP8X4),
+                lhsT_scale=scales[:, t * P : (t + 1) * P],
+                rhs=w_codes[:].bitcast(FP8X4),
+                rhs_scale=w_scales[:],
+                start=True,
+                stop=True,
+            )
+
+        def load(blk, parts):
+            xs = xpool.tile([P, 2 * CH * K], BF16, name="xs")
+            xs_of[blk] = xs
+            n = 2 * CH // parts
+            for i in range(parts):
+                nc.sync.dma_start(
+                    out=xs[:, i * n * K : (i + 1) * n * K].rearrange("p (t k) -> p t k", k=K),
+                    in_=xv[:, blk * 2 * CH + i * n : blk * 2 * CH + (i + 1) * n, :],
+                )
+
+        def transposes(c):
+            xw = xs_of[c // 2][:].bitcast(F32)
+            banks = []
+            for h in range(2):
+                xt = ps_xt.tile([P, 512], F32, name="xt")
+                banks.append(xt)
+                for q in range(4):
+                    loc = (c % 2) * CH + 2 * h + q // 2
+                    w0 = loc * (K // 2)
+                    nc.tensor.transpose(xt[:, q * P : (q + 1) * P], xw[:, w0 + q % 2 : w0 + K // 2 : 2], ident[:])
+            xt_of[c] = banks
+
+        def copies(c, on_scalar):
+            g = gpool.tile([P, CH * K], BF16, name="g", align_bytes=64)
+            g_of[c] = g
+            gw = g[:].bitcast(F32)
+            for h in range(2):
+                dst = gw[:, h * 512 : (h + 1) * 512].rearrange("p (t r u) -> p t r u", t=2, u=2)
+                src = xt_of[c][h][:].rearrange("p (t u r) -> p t r u", t=2, u=2)
+                if h >= 2 - on_scalar:
+                    sc.copy(out=dst, in_=src)
+                else:
+                    v.tensor_copy(out=dst, in_=src)
+
+        def x_squares(c):
+            xs = xs_of[c // 2]
+            calls = []
+            for j in range(CH):
+                loc = (c % 2) * CH + j
+                t = c * CH + j
+                calls.append(act(junk_c[j][:], xs[:, loc * K : (loc + 1) * K], ACT.Square, s2[:, 0, t : t + 1]))
+            return calls
+
+        def quantise(c):
+            t0 = c * CH
+            v.quantize_mx(
+                out=codes[:, t0 * P : (t0 + CH) * P].bitcast(FP8X4),
+                scales=scales[:, t0 * P : (t0 + CH) * P],
+                in_=g_of[c][:],
+            )
+
+        def products(c, pool, name, keep):
+            bank = pool.tile([P, 512], F32, name=name)
+            keep[c] = bank
+            for j in range(CH):
+                mx(bank[:, j * P : (j + 1) * P], c * CH + j)
+
+        def m_squares(c):
+            return [
+                act(junk_d[j][:], ms_of[c][:, j * P : (j + 1) * P], ACT.Square, s2[:, 1, c * CH + j : c * CH + j + 1])
+                for j in range(CH)
+            ]
+
+        def m_dot_b(c):
+            return [
+                stt(
+                    junk_e[j][:],
+                    mv_of[c][:, j * P : (j + 1) * P],
+                    1.0,
+                    b_pos[:],
+                    ALU.mult,
+                    ALU.mult,
+                    pb[:, c * CH + j : c * CH + j + 1],
+                )
+                for j in range(CH)
+            ]
+
+        def store(c):
+            return lambda: nc.sync.dma_start(
+                out=ov[:, (c - 1) * CH : (c + 1) * CH, :],
+                in_=y_of[c // 2][:].rearrange("p (t o) -> p t o", o=DOUT),
+            )
+
+        def finish_scalar(c):
+            t1 = bpool.tile([P, CH * DOUT], F32, name="bb")
+            t1_of[c] = t1
+            return [
+                scaled(t1[:, j * P : (j + 1) * P], m2_of[c][:, j * P : (j + 1) * P], al[:, c * CH + j : c * CH + j + 1])
+                for j in range(CH)
+            ]
+
+        def finish_vector(c, with_scalar):
+            if c % 2 == 0:
+                y_of[c // 2] = ypool.tile([P, 2 * CH * DOUT], F32, name="y")
+            y = y_of[c // 2]
+            off = (c % 2) * CH * DOUT
+            calls = []
+            first = []
+            if with_scalar:
+                t1 = t1_of[c]
+                for j in range(CH):
+                    t = c * CH + j
+                    calls.append(
+                        stt(
+                            y[:, off + j * P : off + (j + 1) * P],
+                            b_neg[:],
+                            nbe[:, t : t + 1],
+                            t1[:, j * P : (j + 1) * P],
+                            ALU.mult,
+                            ALU.add,
+                        )
+                    )
+            else:
+                bb = bpool.tile([P, CH * DOUT], F32, name="bb")
+                for j in range(CH):
+                    t = c * CH + j
+                    first.append(ts(bb[:, j * P : (j + 1) * P], b_neg[:], nbe[:, t : t + 1], None, ALU.mult))
+                for j in range(CH):
+                    t = c * CH + j
+                    calls.append(
+                        stt(
+                            y[:, off + j * P : off + (j + 1) * P],
+                            m2_of[c][:, j * P : (j + 1) * P],
+                            al[:, t : t + 1],
+                            bb[:, j * P : (j + 1) * P],
+                            ALU.mult,
+                            ALU.add,
+                        )
+                    )
+            ysl = y[:, off : off + CH * DOUT]
+            last = [stt(ysl, ysl, 0.2, ysl, ALU.mult, ALU.max)]
+            if c % 2 == 1:
+                last.append(store(c))
+            return first, calls, last
+
+        def chain(a, b):
+            sl = slice(a, b)
+            xn = c_nrm[:, 0, sl]
+            mn = c_nrm[:, 1, sl]
+            rxn = c_rnrm[:, 0, sl]
+            rmn = c_rnrm[:, 1, sl]
+            seg0 = [ts(c_s2c[:, :, sl], s2[:, :, sl], 1e-30, None, ALU.max)]
+            root1 = [act(c_nrm[:, :, sl], c_s2c[:, :, sl], ACT.Sqrt)]
+            seg1 = [
+                rcp(c_rnrm[:, :, sl], c_nrm[:, :, sl]),
+                ts(c_nv[:, sl], xn, 1.0 - 1e-5, -1.0, ALU.min, ALU.mult),
+                tt(c_r[:, sl], mn, rxn, ALU.mult),
+                ts(c_dn[:, sl], c_nv[:, sl], 1.0, None, ALU.add),
+                rcp(c_rdn[:, sl], c_dn[:, sl]),
+                ts(c_base[:, sl], c_rdn[:, sl], 2.0, -1.0, ALU.mult, ALU.add),
+                power(c_e[:, sl], c_base[:, sl], c_r[:, sl]),
+            ]
+            seg2 = [
+                ts(c_e1[:, sl], c_e[:, sl], 1.0, None, ALU.add),
+                rcp(c_re[:, sl], c_e1[:, sl]),
+                ts(c_t[:, sl], c_re[:, sl], -2.0, 1.0, ALU.mult, ALU.add),
+                tt(c_s[:, sl], c_t[:, sl], rmn, ALU.mult),
+                tt(c_x2[:, sl], c_t[:, sl], c_t[:, sl], ALU.mult),
+                tt(c_xy[:, sl], c_s[:, sl], pb[:, sl], ALU.mult),
+                ts(c_c1[:, sl], c_xy[:, sl], 2.0, 1.0, ALU.mult, ALU.add),
+                stt(c_den[:, sl], c_x2[:, sl], y2[:], c_c1[:, sl], ALU.mult, ALU.add),
+                stt(c_num[:, sl], c_x2[:, sl], ym1[:], c_c1[:, sl], ALU.add, ALU.add),
+                ts(c_denc[:, sl], c_den[:, sl], 1e-15, None, ALU.max),
+                stt(c_as[:, sl], c_c1[:, sl], y2[:], c_s[:, sl], ALU.add, ALU.mult),
+                rcp(c_rden[:, sl], c_denc[:, sl]),
+                tt(c_nn2[:, sl], c_num[:, sl], c_rden[:, sl], ALU.mult),
+                ts(c_nn2c[:, sl], c_nn2[:, sl], 1e-30, None, ALU.max),
+            ]
+            root2 = [act(c_nn[:, sl], c_nn2c[:, sl], ACT.Sqrt)]
+            seg3 = [
+                rcp(c_rnn[:, sl], c_nn[:, sl]),
+                ts(c_f[:, sl], c_rnn[:, sl], 0.999, 1.0, ALU.mult, ALU.min),
+                tt(c_rf[:, sl], c_rden[:, sl], c_f[:, sl], ALU.mult),
+                tt(al[:, sl], c_as[:, sl], c_rf[:, sl], ALU.mult),
+                stt(nbe[:, sl], c_x2[:, sl], 1.0, c_rf[:, sl], ALU.subtract, ALU.mult),
+            ]
+            return seg0, root1, seg1, seg2, root2, seg3
+
+        first_v = {}
+        mid_s = {}
+        late_v = {}
+        avail = [0] * NCH
+        a = 0
+        for n in GROUPS:
+            b = a + n
+            s01 = b // CH - 1 + 3
+            s_2 = s01 + (3 if n >= 32 else 2)
+            s_3 = s_2 + 1
+            seg0, root1, seg1, seg2, root2, seg3 = chain(a, b)
+            first_v[s01] = first_v.get(s01, []) + seg0
+            mid_s[s01] = mid_s.get(s01, []) + root1
+            late_v[s01] = late_v.get(s01, []) + seg1
+            late_v[s_2] = late_v.get(s_2, []) + seg2
+            mid_s[s_3] = mid_s.get(s_3, []) + root2
+            late_v[s_3] = late_v.get(s_3, []) + seg3
+            for c in range(a // CH, b // CH):
+                avail[c] = s_3 + 1
+            a = b
+        p2 = []
+        done = 0
+        while done < NCH:
+            s = len(p2)
+            cap = 1 if s < NCH else 2
+            now = []
+            while len(now) < cap and done < NCH and avail[done] <= s:
+                now.append(done)
+                done += 1
+            p2.append(now)
+        p2.append([])
+
+        make_identity(nc, ident[:])
+        v.memset(half[:], 0.5)
+        sc.dma_start(out=bias_bc[:], in_=bias.partition_broadcast(P))
+        load(0, 2)
+        nc.sync.dma_start(out=w_raw[:], in_=weight)
+        for blk in range(1, LOOKAHEAD):
+            load(blk, 1)
+        transposes(0)
+        w_bank = ps_ms.tile([P, 512], F32, name="ms")
+        w_words = w_raw[:].bitcast(F32)
+        for u in range(2):
+            nc.tensor.transpose(w_bank[:, u * P : (u + 1) * P], w_words[:, u : K // 2 : 2], ident[:])
+        v.tensor_scalar(out=u_f[:], in0=bias_bc[:], scalar1=0.1, scalar2=None, op0=ALU.mult)
+        sc.activation(out=junk_d[0][:], in_=u_f[:], func=ACT.Square, accum_out=un2[:])
+        first_v[0] = [
+            ts(un2c[:], un2[:], 1e-30, None, ALU.max),
+            power(un[:], un2c[:], half[:]),
+            ts(
+                w_grouped[:].rearrange("p (o u e) -> p o u e", u=2, e=2),
+                w_bank[:, 0 : 2 * P].bitcast(BF16).rearrange("p (u o e) -> p o u e", u=2, e=2),
+                0.1,
+                None,
+                ALU.mult,
+            ),
+            lambda: v.quantize_mx(out=w_codes[:].bitcast(FP8X4), scales=w_scales[:], in_=w_grouped[:]),
+            rcp(run[:], un[:]),
+        ]
+        mid_s[0] = [act(th[:], un[:], ACT.Tanh)]
+        late_v[0] = [
+            tt(kk[:], th[:], run[:], ALU.mult),
+            ts(b_pos[:], u_f[:], kk[:], None, ALU.mult),
+            ts(b_neg[:], u_f[:], kk[:], -1.0, ALU.mult, ALU.mult),
+        ]
+        mid_s[1] = [act(junk_d[1][:], b_pos[:], ACT.Square, y2[:])]
+        late_v[1] = [ts(ym1[:], y2[:], -1.0, None, ALU.add)]
+
+        pending = []
+        for s in range(len(p2) - 1):
+            tail = s >= NCH
+            if s % 2 == 0 and s // 2 + LOOKAHEAD < NCH // 2:
+                load(s // 2 + LOOKAHEAD, 1)
+            if s < NCH:
+                copies(s, len(p2[s]))
+            for f in first_v.get(s, []):
+                f()
+            s_calls = []
+            if s < NCH:
+                s_calls += x_squares(s)
+            if 0 <= s - 2 < NCH:
+                s_calls += m_squares(s - 2)
+            if tail:
+                for c in p2[s]:
+                    s_calls += finish_scalar(c)
+            weave(s_calls[:1], [], 0)
+            for f in mid_s.get(s, []):
+                f()
+            weave(s_calls[1:], [], 0)
+            if 0 <= s - 1 < NCH:
+                quantise(s - 1)
+            if s + 1 < NCH:
+                transposes(s + 1)
+            if 0 <= s - 1 < NCH:
+                products(s - 1, ps_ms, "ms", ms_of)
+                products(s - 1, ps_mv, "mv", mv_of)
+            v_calls = []
+            dots = m_dot_b(s - 2) if 0 <= s - 2 < NCH else []
+            for c in p2[s]:
+                first, second, last = finish_vector(c, tail)
+                v_calls += first + pending + dots + second
+                pending = last
+                dots = []
+            v_calls += dots
+            if s == len(p2) - 2:
+                v_calls += pending
+            weave(v_calls, late_v.get(s, []), 2)
+            for c in p2[s + 1]:
+                products(c, ps_m2, "m2", m2_of)

@@ -19,7 +19,7 @@ DOUT = 128
 NT = 128
 CH = 4
 NCH = NT // CH
-GROUPS = (32, 32, 32, 16, 8, 8)
+GROUPS = (16, 16, 16, 16, 16, 16, 16, 8, 8)
 LOOKAHEAD = 4
 
 
@@ -31,7 +31,7 @@ def tile_hypequalizedlinear_t_kernel(tc, x, weight, bias, out):
         const = ctx.enter_context(tc.tile_pool(name="const", bufs=1))
         xpool = ctx.enter_context(tc.tile_pool(name="xpool", bufs=6))
         gpool = ctx.enter_context(tc.tile_pool(name="gpool", bufs=3))
-        bpool = ctx.enter_context(tc.tile_pool(name="bpool", bufs=3))
+        bpool = ctx.enter_context(tc.tile_pool(name="bpool", bufs=4))
         ypool = ctx.enter_context(tc.tile_pool(name="ypool", bufs=4))
         ps_xt = ctx.enter_context(tc.psum_pool(name="ps_xt", bufs=2))
         ps_ms = ctx.enter_context(tc.psum_pool(name="ps_ms", bufs=2))
@@ -41,6 +41,7 @@ def tile_hypequalizedlinear_t_kernel(tc, x, weight, bias, out):
         ctx.enter_context(tc.manual_schedule())
         v = nc.vector
         sc = nc.scalar
+        g_ = nc.gpsimd
 
         def col(name):
             return const.tile([P, 1], F32, name=name)
@@ -55,6 +56,7 @@ def tile_hypequalizedlinear_t_kernel(tc, x, weight, bias, out):
         w_raw = const.tile([P, K], BF16, name="w_raw")
         bias_bc = const.tile([P, DOUT], BF16, name="bias_bc")
         junk_c = [const.tile([P, K], BF16, name="junk_c%d" % i) for i in range(4)]
+        junk_v = [const.tile([P, K], BF16, name="junk_v%d" % i) for i in range(4)]
         junk_d = [const.tile([P, DOUT], F32, name="junk_d%d" % i) for i in range(4)]
         junk_e = [const.tile([P, DOUT], F32, name="junk_e%d" % i) for i in range(4)]
         w_grouped = const.tile([P, K], BF16, name="w_grouped", align_bytes=64)
@@ -62,7 +64,6 @@ def tile_hypequalizedlinear_t_kernel(tc, x, weight, bias, out):
         w_scales = const.tile([P, DOUT], U8, name="w_scales", align_bytes=64)
         u_f = const.tile([P, DOUT], F32, name="u_f")
         b_pos = const.tile([P, DOUT], F32, name="b_pos")
-        b_neg = const.tile([P, DOUT], F32, name="b_neg")
         un2 = col("un2")
         un2c = col("un2c")
         un = col("un")
@@ -70,18 +71,15 @@ def tile_hypequalizedlinear_t_kernel(tc, x, weight, bias, out):
         run = col("run")
         kk = col("kk")
         y2 = col("y2")
-        ym1 = col("ym1")
+        y2p1 = col("y2p1")
         codes = const.tile([P, NT * P], U32, name="codes", align_bytes=64)
         scales = const.tile([P, NT * P], U8, name="scales", align_bytes=64)
         s2 = wide("s2", 2)
         pb = wide("pb")
         al = wide("al")
-        nbe = wide("nbe")
-        c_s2c = wide("c_s2c", 2)
         c_nrm = wide("c_nrm", 2)
         c_rnrm = wide("c_rnrm", 2)
-        c_nv = wide("c_nv")
-        c_dn = wide("c_dn")
+        c_ndn = wide("c_ndn")
         c_rdn = wide("c_rdn")
         c_base = wide("c_base")
         c_r = wide("c_r")
@@ -91,17 +89,14 @@ def tile_hypequalizedlinear_t_kernel(tc, x, weight, bias, out):
         c_t = wide("c_t")
         c_s = wide("c_s")
         c_x2 = wide("c_x2")
+        c_x1 = wide("c_x1")
         c_xy = wide("c_xy")
-        c_c1 = wide("c_c1")
+        c_d0 = wide("c_d0")
         c_den = wide("c_den")
-        c_denc = wide("c_denc")
-        c_rden = wide("c_rden")
         c_num = wide("c_num")
-        c_nn2 = wide("c_nn2")
-        c_nn2c = wide("c_nn2c")
-        c_nn = wide("c_nn")
-        c_rnn = wide("c_rnn")
-        c_f = wide("c_f")
+        c_nd = wide("c_nd")
+        c_q = wide("c_q")
+        c_mx = wide("c_mx")
         c_rf = wide("c_rf")
         c_as = wide("c_as")
 
@@ -111,7 +106,7 @@ def tile_hypequalizedlinear_t_kernel(tc, x, weight, bias, out):
         ms_of = {}
         mv_of = {}
         m2_of = {}
-        t1_of = {}
+        bb_of = {}
         y_of = {}
 
         def ts(o, i, s1, s2_, o0, o1=None):
@@ -128,24 +123,25 @@ def tile_hypequalizedlinear_t_kernel(tc, x, weight, bias, out):
         def rcp(o, i):
             return lambda: v.reciprocal(out=o, in_=i)
 
-        def act(o, i, func, acc=None):
-            return lambda: sc.activation(out=o, in_=i, func=func, accum_out=acc)
+        def act(o, i, func, acc=None, add=0.0):
+            return lambda: sc.activation(out=o, in_=i, func=func, bias=add, accum_out=acc)
 
-        def scaled(o, i, s):
-            return lambda: sc.activation(out=o, in_=i, func=ACT.Copy, scale=s)
+        def gts(o, i, s1, s2_, o0, o1):
+            return lambda: g_.tensor_scalar(out=o, in0=i, scalar1=s1, scalar2=s2_, op0=o0, op1=o1)
 
-        def power(o, i0, i1):
-            return lambda: nc.gpsimd.tensor_tensor(out=o, in0=i0, in1=i1, op=ALU.pow)
+        def gtt(o, i0, i1, op):
+            return lambda: g_.tensor_tensor(out=o, in0=i0, in1=i1, op=op)
 
-        def weave(bulk, extra, skip):
+        def weave(bulk, extras):
+            order = sorted(extras, key=lambda e: e[0])
             i = 0
             for n, f in enumerate(bulk):
-                f()
-                if n >= skip and n % 2 == 0 and i < len(extra):
-                    extra[i]()
+                while i < len(order) and order[i][0] * len(bulk) <= n and (len(bulk) > CH or order[i][0] < 0.5):
+                    order[i][1]()
                     i += 1
-            for f in extra[i:]:
                 f()
+            for e in order[i:]:
+                e[1]()
 
         def mx(dst, t):
             nc.tensor.matmul_mx(
@@ -192,14 +188,20 @@ def tile_hypequalizedlinear_t_kernel(tc, x, weight, bias, out):
                 else:
                     v.tensor_copy(out=dst, in_=src)
 
-        def x_squares(c):
+        def x_squares(c, n_v):
             xs = xs_of[c // 2]
             calls = []
+            v_calls = []
             for j in range(CH):
                 loc = (c % 2) * CH + j
                 t = c * CH + j
-                calls.append(act(junk_c[j][:], xs[:, loc * K : (loc + 1) * K], ACT.Square, s2[:, 0, t : t + 1]))
-            return calls
+                xt_ = xs[:, loc * K : (loc + 1) * K]
+                acc = s2[:, 0, t : t + 1]
+                if j < CH - n_v:
+                    calls.append(act(junk_c[j][:], xt_, ACT.Square, acc))
+                else:
+                    v_calls.append(stt(junk_v[j][:], xt_, 1.0, xt_, ALU.mult, ALU.mult, acc))
+            return calls, v_calls
 
         def quantise(c):
             t0 = c * CH
@@ -226,7 +228,7 @@ def tile_hypequalizedlinear_t_kernel(tc, x, weight, bias, out):
                 stt(
                     junk_e[j][:],
                     mv_of[c][:, j * P : (j + 1) * P],
-                    1.0,
+                    2.0,
                     b_pos[:],
                     ALU.mult,
                     ALU.mult,
@@ -241,57 +243,36 @@ def tile_hypequalizedlinear_t_kernel(tc, x, weight, bias, out):
                 in_=y_of[c // 2][:].rearrange("p (t o) -> p t o", o=DOUT),
             )
 
-        def finish_scalar(c):
-            t1 = bpool.tile([P, CH * DOUT], F32, name="bb")
-            t1_of[c] = t1
-            return [
-                scaled(t1[:, j * P : (j + 1) * P], m2_of[c][:, j * P : (j + 1) * P], al[:, c * CH + j : c * CH + j + 1])
-                for j in range(CH)
-            ]
+        def bias_terms(c):
+            bb = bpool.tile([P, CH * DOUT], F32, name="bb")
+            bb_of[c] = bb
+            for j in range(CH):
+                t = c * CH + j
+                gts(bb[:, j * P : (j + 1) * P], b_pos[:], c_x1[:, t : t + 1], c_rf[:, t : t + 1], ALU.mult, ALU.mult)()
 
-        def finish_vector(c, with_scalar):
+        def finish(c):
             if c % 2 == 0:
                 y_of[c // 2] = ypool.tile([P, 2 * CH * DOUT], F32, name="y")
             y = y_of[c // 2]
             off = (c % 2) * CH * DOUT
             calls = []
-            first = []
-            if with_scalar:
-                t1 = t1_of[c]
-                for j in range(CH):
-                    t = c * CH + j
-                    calls.append(
-                        stt(
-                            y[:, off + j * P : off + (j + 1) * P],
-                            b_neg[:],
-                            nbe[:, t : t + 1],
-                            t1[:, j * P : (j + 1) * P],
-                            ALU.mult,
-                            ALU.add,
-                        )
+            for j in range(CH):
+                t = c * CH + j
+                calls.append(
+                    stt(
+                        y[:, off + j * P : off + (j + 1) * P],
+                        m2_of[c][:, j * P : (j + 1) * P],
+                        al[:, t : t + 1],
+                        bb_of[c][:, j * P : (j + 1) * P],
+                        ALU.mult,
+                        ALU.add,
                     )
-            else:
-                bb = bpool.tile([P, CH * DOUT], F32, name="bb")
-                for j in range(CH):
-                    t = c * CH + j
-                    first.append(ts(bb[:, j * P : (j + 1) * P], b_neg[:], nbe[:, t : t + 1], None, ALU.mult))
-                for j in range(CH):
-                    t = c * CH + j
-                    calls.append(
-                        stt(
-                            y[:, off + j * P : off + (j + 1) * P],
-                            m2_of[c][:, j * P : (j + 1) * P],
-                            al[:, t : t + 1],
-                            bb[:, j * P : (j + 1) * P],
-                            ALU.mult,
-                            ALU.add,
-                        )
-                    )
+                )
             ysl = y[:, off : off + CH * DOUT]
             last = [stt(ysl, ysl, 0.2, ysl, ALU.mult, ALU.max)]
             if c % 2 == 1:
                 last.append(store(c))
-            return first, calls, last
+            return calls, last
 
         def chain(a, b):
             sl = slice(a, b)
@@ -299,62 +280,65 @@ def tile_hypequalizedlinear_t_kernel(tc, x, weight, bias, out):
             mn = c_nrm[:, 1, sl]
             rxn = c_rnrm[:, 0, sl]
             rmn = c_rnrm[:, 1, sl]
-            seg0 = [ts(c_s2c[:, :, sl], s2[:, :, sl], 1e-30, None, ALU.max)]
-            root1 = [act(c_nrm[:, :, sl], c_s2c[:, :, sl], ACT.Sqrt)]
-            seg1 = [
-                rcp(c_rnrm[:, :, sl], c_nrm[:, :, sl]),
-                ts(c_nv[:, sl], xn, 1.0 - 1e-5, -1.0, ALU.min, ALU.mult),
-                tt(c_r[:, sl], mn, rxn, ALU.mult),
-                ts(c_dn[:, sl], c_nv[:, sl], 1.0, None, ALU.add),
-                rcp(c_rdn[:, sl], c_dn[:, sl]),
-                ts(c_base[:, sl], c_rdn[:, sl], 2.0, -1.0, ALU.mult, ALU.add),
-                power(c_e[:, sl], c_base[:, sl], c_r[:, sl]),
+            s_root = act(c_nrm[:, :, sl], s2[:, :, sl], ACT.Sqrt, add=1e-30)
+            g_ndn = gts(c_ndn[:, sl], xn, 1.0 - 1e-5, 1.0, ALU.min, ALU.subtract)
+            v_rnrm = rcp(c_rnrm[:, :, sl], c_nrm[:, :, sl])
+            v_rdn = rcp(c_rdn[:, sl], c_ndn[:, sl])
+            g_pow = [
+                gtt(c_r[:, sl], mn, rxn, ALU.mult),
+                gts(c_base[:, sl], c_rdn[:, sl], -2.0, -1.0, ALU.mult, ALU.add),
+                gtt(c_e[:, sl], c_base[:, sl], c_r[:, sl], ALU.pow),
+                gts(c_e1[:, sl], c_e[:, sl], 1.0, 1.0, ALU.mult, ALU.add),
             ]
-            seg2 = [
-                ts(c_e1[:, sl], c_e[:, sl], 1.0, None, ALU.add),
-                rcp(c_re[:, sl], c_e1[:, sl]),
+            v_re = rcp(c_re[:, sl], c_e1[:, sl])
+            v_mid = [
                 ts(c_t[:, sl], c_re[:, sl], -2.0, 1.0, ALU.mult, ALU.add),
                 tt(c_s[:, sl], c_t[:, sl], rmn, ALU.mult),
                 tt(c_x2[:, sl], c_t[:, sl], c_t[:, sl], ALU.mult),
                 tt(c_xy[:, sl], c_s[:, sl], pb[:, sl], ALU.mult),
-                ts(c_c1[:, sl], c_xy[:, sl], 2.0, 1.0, ALU.mult, ALU.add),
-                stt(c_den[:, sl], c_x2[:, sl], y2[:], c_c1[:, sl], ALU.mult, ALU.add),
-                stt(c_num[:, sl], c_x2[:, sl], ym1[:], c_c1[:, sl], ALU.add, ALU.add),
-                ts(c_denc[:, sl], c_den[:, sl], 1e-15, None, ALU.max),
-                stt(c_as[:, sl], c_c1[:, sl], y2[:], c_s[:, sl], ALU.add, ALU.mult),
-                rcp(c_rden[:, sl], c_denc[:, sl]),
-                tt(c_nn2[:, sl], c_num[:, sl], c_rden[:, sl], ALU.mult),
-                ts(c_nn2c[:, sl], c_nn2[:, sl], 1e-30, None, ALU.max),
+                stt(c_d0[:, sl], c_x2[:, sl], y2[:], c_xy[:, sl], ALU.mult, ALU.add),
+                stt(c_num[:, sl], c_x2[:, sl], y2[:], c_xy[:, sl], ALU.add, ALU.add),
+                ts(c_den[:, sl], c_d0[:, sl], 1.0, 1e-15, ALU.add, ALU.max),
+                stt(c_as[:, sl], c_xy[:, sl], y2p1[:], c_s[:, sl], ALU.add, ALU.mult),
+                stt(c_nd[:, sl], c_num[:, sl], 0.0, c_den[:, sl], ALU.max, ALU.mult),
             ]
-            root2 = [act(c_nn[:, sl], c_nn2c[:, sl], ACT.Sqrt)]
-            seg3 = [
-                rcp(c_rnn[:, sl], c_nn[:, sl]),
-                ts(c_f[:, sl], c_rnn[:, sl], 0.999, 1.0, ALU.mult, ALU.min),
-                tt(c_rf[:, sl], c_rden[:, sl], c_f[:, sl], ALU.mult),
-                tt(al[:, sl], c_as[:, sl], c_rf[:, sl], ALU.mult),
-                stt(nbe[:, sl], c_x2[:, sl], 1.0, c_rf[:, sl], ALU.subtract, ALU.mult),
-            ]
-            return seg0, root1, seg1, seg2, root2, seg3
+            g_x1 = gts(c_x1[:, sl], c_x2[:, sl], -1.0, 1.0, ALU.mult, ALU.add)
+            s_q = lambda: sc.activation(out=c_q[:, sl], in_=c_nd[:, sl], func=ACT.Sqrt, scale=1.0 / (0.999 * 0.999))
+            v_mx = tt(c_mx[:, sl], c_den[:, sl], c_q[:, sl], ALU.max)
+            v_rf = rcp(c_rf[:, sl], c_mx[:, sl])
+            g_al = gtt(al[:, sl], c_as[:, sl], c_rf[:, sl], ALU.mult)
+            return s_root, g_ndn, v_rnrm, v_rdn, g_pow, v_re, v_mid, g_x1, s_q, v_mx, v_rf, g_al
 
-        first_v = {}
-        mid_s = {}
-        late_v = {}
+        ex_v = {}
+        ex_s = {}
+        ex_g = {}
+
+        def put(plan, s, f, call):
+            plan.setdefault(s, []).append((f, call))
+
         avail = [0] * NCH
         a = 0
         for n in GROUPS:
             b = a + n
-            s01 = b // CH - 1 + 3
-            s_2 = s01 + (3 if n >= 32 else 2)
-            s_3 = s_2 + 1
-            seg0, root1, seg1, seg2, root2, seg3 = chain(a, b)
-            first_v[s01] = first_v.get(s01, []) + seg0
-            mid_s[s01] = mid_s.get(s01, []) + root1
-            late_v[s01] = late_v.get(s01, []) + seg1
-            late_v[s_2] = late_v.get(s_2, []) + seg2
-            mid_s[s_3] = mid_s.get(s_3, []) + root2
-            late_v[s_3] = late_v.get(s_3, []) + seg3
+            e = b // CH + 1
+            w = 1 if n > 8 else 0
+            s_root, g_ndn, v_rnrm, v_rdn, g_pow, v_re, v_mid, g_x1, s_q, v_mx, v_rf, g_al = chain(a, b)
+            put(ex_s, e, 0.7, s_root)
+            put(ex_g, e, 0.0, g_ndn)
+            put(ex_v, e, 0.95, v_rnrm)
+            put(ex_v, e + 1, 0.3, v_rdn)
+            for call in g_pow:
+                put(ex_g, e + 1, 0.0, call)
+            put(ex_v, e + 2 + w, 0.05 if w else 0.4, v_re)
+            for i, call in enumerate(v_mid):
+                put(ex_v, e + 2 + w, (0.15 if w else 0.5) + 0.06 * i, call)
+            put(ex_g, e + 2 + w, 0.0, g_x1)
+            put(ex_s, e + 3 + w, 0.15, s_q)
+            put(ex_v, e + 3 + w, 0.4, v_mx)
+            put(ex_v, e + 3 + w, 0.55, v_rf)
+            put(ex_g, e + 3 + w, 0.0, g_al)
             for c in range(a // CH, b // CH):
-                avail[c] = s_3 + 1
+                avail[c] = e + 4 + w
             a = b
         p2 = []
         done = 0
@@ -382,31 +366,29 @@ def tile_hypequalizedlinear_t_kernel(tc, x, weight, bias, out):
             nc.tensor.transpose(w_bank[:, u * P : (u + 1) * P], w_words[:, u : K // 2 : 2], ident[:])
         v.tensor_scalar(out=u_f[:], in0=bias_bc[:], scalar1=0.1, scalar2=None, op0=ALU.mult)
         sc.activation(out=junk_d[0][:], in_=u_f[:], func=ACT.Square, accum_out=un2[:])
-        first_v[0] = [
-            ts(un2c[:], un2[:], 1e-30, None, ALU.max),
-            power(un[:], un2c[:], half[:]),
-            ts(
-                w_grouped[:].rearrange("p (o u e) -> p o u e", u=2, e=2),
-                w_bank[:, 0 : 2 * P].bitcast(BF16).rearrange("p (u o e) -> p o u e", u=2, e=2),
-                0.1,
-                None,
-                ALU.mult,
-            ),
-            lambda: v.quantize_mx(out=w_codes[:].bitcast(FP8X4), scales=w_scales[:], in_=w_grouped[:]),
-            rcp(run[:], un[:]),
-        ]
-        mid_s[0] = [act(th[:], un[:], ACT.Tanh)]
-        late_v[0] = [
-            tt(kk[:], th[:], run[:], ALU.mult),
-            ts(b_pos[:], u_f[:], kk[:], None, ALU.mult),
-            ts(b_neg[:], u_f[:], kk[:], -1.0, ALU.mult, ALU.mult),
-        ]
-        mid_s[1] = [act(junk_d[1][:], b_pos[:], ACT.Square, y2[:])]
-        late_v[1] = [ts(ym1[:], y2[:], -1.0, None, ALU.add)]
+        first_v = {
+            0: [
+                ts(un2c[:], un2[:], 1e-30, None, ALU.max),
+                gtt(un[:], un2c[:], half[:], ALU.pow),
+                ts(
+                    w_grouped[:].rearrange("p (o u e) -> p o u e", u=2, e=2),
+                    w_bank[:, 0 : 2 * P].bitcast(BF16).rearrange("p (u o e) -> p o u e", u=2, e=2),
+                    0.1,
+                    None,
+                    ALU.mult,
+                ),
+                lambda: v.quantize_mx(out=w_codes[:].bitcast(FP8X4), scales=w_scales[:], in_=w_grouped[:]),
+                rcp(run[:], un[:]),
+            ]
+        }
+        put(ex_s, 0, 0.3, act(th[:], un[:], ACT.Tanh))
+        put(ex_v, 0, 0.0, tt(kk[:], th[:], run[:], ALU.mult))
+        put(ex_v, 0, 0.0, ts(b_pos[:], u_f[:], kk[:], None, ALU.mult))
+        put(ex_s, 1, 0.3, act(junk_d[1][:], b_pos[:], ACT.Square, y2[:]))
+        put(ex_v, 2, 0.0, ts(y2p1[:], y2[:], 1.0, None, ALU.add))
 
         pending = []
         for s in range(len(p2) - 1):
-            tail = s >= NCH
             if s % 2 == 0 and s // 2 + LOOKAHEAD < NCH // 2:
                 load(s // 2 + LOOKAHEAD, 1)
             if s < NCH:
@@ -414,17 +396,13 @@ def tile_hypequalizedlinear_t_kernel(tc, x, weight, bias, out):
             for f in first_v.get(s, []):
                 f()
             s_calls = []
-            if s < NCH:
-                s_calls += x_squares(s)
+            v_squares = []
             if 0 <= s - 2 < NCH:
                 s_calls += m_squares(s - 2)
-            if tail:
-                for c in p2[s]:
-                    s_calls += finish_scalar(c)
-            weave(s_calls[:1], [], 0)
-            for f in mid_s.get(s, []):
-                f()
-            weave(s_calls[1:], [], 0)
+            if s < NCH:
+                calls, v_squares = x_squares(s, 1 if not p2[s] and s % 2 == 1 else 0)
+                s_calls += calls
+            weave(s_calls, ex_s.get(s, []))
             if 0 <= s - 1 < NCH:
                 quantise(s - 1)
             if s + 1 < NCH:
@@ -432,16 +410,18 @@ def tile_hypequalizedlinear_t_kernel(tc, x, weight, bias, out):
             if 0 <= s - 1 < NCH:
                 products(s - 1, ps_ms, "ms", ms_of)
                 products(s - 1, ps_mv, "mv", mv_of)
-            v_calls = []
+            v_calls = v_squares
             dots = m_dot_b(s - 2) if 0 <= s - 2 < NCH else []
             for c in p2[s]:
-                first, second, last = finish_vector(c, tail)
-                v_calls += first + pending + dots + second
+                calls, last = finish(c)
+                v_calls += pending + dots + calls
                 pending = last
                 dots = []
             v_calls += dots
             if s == len(p2) - 2:
                 v_calls += pending
-            weave(v_calls, late_v.get(s, []), 2)
+            weave(v_calls, ex_v.get(s, []))
+            weave([], ex_g.get(s, []))
             for c in p2[s + 1]:
+                bias_terms(c)
                 products(c, ps_m2, "m2", m2_of)

@@ -20,6 +20,7 @@ NT = 128
 CH = 4
 NCH = NT // CH
 GROUPS = (16, 16, 16, 16, 16, 16, 16, 8, 8)
+POW_COLS = 8
 LOOKAHEAD = 4
 
 
@@ -77,10 +78,8 @@ def tile_hypequalizedlinear_t_kernel(tc, x, weight, bias, out):
         s2 = wide("s2", 2)
         pb = wide("pb")
         al = wide("al")
-        c_nrm = wide("c_nrm", 2)
-        c_rnrm = wide("c_rnrm", 2)
-        c_ndn = wide("c_ndn")
-        c_rdn = wide("c_rdn")
+        c_nrm = wide("c_nrm", 3)
+        c_rnrm = wide("c_rnrm", 3)
         c_base = wide("c_base")
         c_r = wide("c_r")
         c_e = wide("c_e")
@@ -126,9 +125,6 @@ def tile_hypequalizedlinear_t_kernel(tc, x, weight, bias, out):
         def act(o, i, func, acc=None, add=0.0):
             return lambda: sc.activation(out=o, in_=i, func=func, bias=add, accum_out=acc)
 
-        def gts(o, i, s1, s2_, o0, o1):
-            return lambda: g_.tensor_scalar(out=o, in0=i, scalar1=s1, scalar2=s2_, op0=o0, op1=o1)
-
         def gtt(o, i0, i1, op):
             return lambda: g_.tensor_tensor(out=o, in0=i0, in1=i1, op=op)
 
@@ -136,7 +132,7 @@ def tile_hypequalizedlinear_t_kernel(tc, x, weight, bias, out):
             order = sorted(extras, key=lambda e: e[0])
             i = 0
             for n, f in enumerate(bulk):
-                while i < len(order) and order[i][0] * len(bulk) <= n and (len(bulk) > CH or order[i][0] < 0.5):
+                while i < len(order) and order[i][0] * len(bulk) <= n:
                     order[i][1]()
                     i += 1
                 f()
@@ -246,9 +242,13 @@ def tile_hypequalizedlinear_t_kernel(tc, x, weight, bias, out):
         def bias_terms(c):
             bb = bpool.tile([P, CH * DOUT], F32, name="bb")
             bb_of[c] = bb
+            calls = []
             for j in range(CH):
                 t = c * CH + j
-                gts(bb[:, j * P : (j + 1) * P], b_pos[:], c_x1[:, t : t + 1], c_rf[:, t : t + 1], ALU.mult, ALU.mult)()
+                calls.append(
+                    ts(bb[:, j * P : (j + 1) * P], b_pos[:], c_x1[:, t : t + 1], c_rf[:, t : t + 1], ALU.mult, ALU.mult)
+                )
+            return calls
 
         def finish(c):
             if c % 2 == 0:
@@ -274,69 +274,75 @@ def tile_hypequalizedlinear_t_kernel(tc, x, weight, bias, out):
                 last.append(store(c))
             return calls, last
 
+        def powers(i):
+            sl = slice(i, i + POW_COLS)
+            return (
+                ts(c_base[:, sl], c_rnrm[:, 2, sl], -2.0, -1.0, ALU.mult, ALU.add),
+                gtt(c_e[:, sl], c_base[:, sl], c_r[:, sl], ALU.pow),
+            )
+
         def chain(a, b):
             sl = slice(a, b)
-            xn = c_nrm[:, 0, sl]
-            mn = c_nrm[:, 1, sl]
             rxn = c_rnrm[:, 0, sl]
             rmn = c_rnrm[:, 1, sl]
-            s_root = act(c_nrm[:, :, sl], s2[:, :, sl], ACT.Sqrt, add=1e-30)
-            g_ndn = gts(c_ndn[:, sl], xn, 1.0 - 1e-5, 1.0, ALU.min, ALU.subtract)
-            v_rnrm = rcp(c_rnrm[:, :, sl], c_nrm[:, :, sl])
-            v_rdn = rcp(c_rdn[:, sl], c_ndn[:, sl])
-            g_pow = [
-                gtt(c_r[:, sl], mn, rxn, ALU.mult),
-                gts(c_base[:, sl], c_rdn[:, sl], -2.0, -1.0, ALU.mult, ALU.add),
-                gtt(c_e[:, sl], c_base[:, sl], c_r[:, sl], ALU.pow),
-                gts(c_e1[:, sl], c_e[:, sl], 1.0, 1.0, ALU.mult, ALU.add),
+            s_root = act(c_nrm[:, 0:2, sl], s2[:, :, sl], ACT.Sqrt, add=1e-30)
+            v_ndn = ts(c_nrm[:, 2, sl], c_nrm[:, 0, sl], 1.0 - 1e-5, 1.0, ALU.min, ALU.subtract)
+            v_r = [
+                rcp(c_rnrm[:, :, sl], c_nrm[:, :, sl]),
+                tt(c_r[:, sl], c_nrm[:, 1, sl], rxn, ALU.mult),
             ]
-            v_re = rcp(c_re[:, sl], c_e1[:, sl])
             v_mid = [
+                ts(c_e1[:, sl], c_e[:, sl], 1.0, None, ALU.add),
+                rcp(c_re[:, sl], c_e1[:, sl]),
                 ts(c_t[:, sl], c_re[:, sl], -2.0, 1.0, ALU.mult, ALU.add),
                 tt(c_s[:, sl], c_t[:, sl], rmn, ALU.mult),
                 tt(c_x2[:, sl], c_t[:, sl], c_t[:, sl], ALU.mult),
                 tt(c_xy[:, sl], c_s[:, sl], pb[:, sl], ALU.mult),
+                ts(c_x1[:, sl], c_x2[:, sl], -1.0, 1.0, ALU.mult, ALU.add),
                 stt(c_d0[:, sl], c_x2[:, sl], y2[:], c_xy[:, sl], ALU.mult, ALU.add),
                 stt(c_num[:, sl], c_x2[:, sl], y2[:], c_xy[:, sl], ALU.add, ALU.add),
                 ts(c_den[:, sl], c_d0[:, sl], 1.0, 1e-15, ALU.add, ALU.max),
                 stt(c_as[:, sl], c_xy[:, sl], y2p1[:], c_s[:, sl], ALU.add, ALU.mult),
                 stt(c_nd[:, sl], c_num[:, sl], 0.0, c_den[:, sl], ALU.max, ALU.mult),
             ]
-            g_x1 = gts(c_x1[:, sl], c_x2[:, sl], -1.0, 1.0, ALU.mult, ALU.add)
-            s_q = lambda: sc.activation(out=c_q[:, sl], in_=c_nd[:, sl], func=ACT.Sqrt, scale=1.0 / (0.999 * 0.999))
-            v_mx = tt(c_mx[:, sl], c_den[:, sl], c_q[:, sl], ALU.max)
-            v_rf = rcp(c_rf[:, sl], c_mx[:, sl])
-            g_al = gtt(al[:, sl], c_as[:, sl], c_rf[:, sl], ALU.mult)
-            return s_root, g_ndn, v_rnrm, v_rdn, g_pow, v_re, v_mid, g_x1, s_q, v_mx, v_rf, g_al
+
+            def s_q():
+                sc.activation(out=c_q[:, sl], in_=c_nd[:, sl], func=ACT.Sqrt, scale=1.0 / (0.999 * 0.999))
+
+            v_end = [
+                tt(c_mx[:, sl], c_den[:, sl], c_q[:, sl], ALU.max),
+                rcp(c_rf[:, sl], c_mx[:, sl]),
+                tt(al[:, sl], c_as[:, sl], c_rf[:, sl], ALU.mult),
+            ]
+            return s_root, v_ndn, v_r, v_mid, s_q, v_end
 
         ex_v = {}
-        ex_s = {}
-        ex_g = {}
+        end_v = {}
+        gate = {}
+        root = {}
+        early_s = {}
 
-        def put(plan, s, f, call):
-            plan.setdefault(s, []).append((f, call))
+        def put(s, f, call):
+            ex_v.setdefault(s, []).append((f, call))
 
         avail = [0] * NCH
         a = 0
         for n in GROUPS:
             b = a + n
             e = b // CH + 1
-            w = 1 if n > 8 else 0
-            s_root, g_ndn, v_rnrm, v_rdn, g_pow, v_re, v_mid, g_x1, s_q, v_mx, v_rf, g_al = chain(a, b)
-            put(ex_s, e, 0.7, s_root)
-            put(ex_g, e, 0.0, g_ndn)
-            put(ex_v, e, 0.95, v_rnrm)
-            put(ex_v, e + 1, 0.3, v_rdn)
-            for call in g_pow:
-                put(ex_g, e + 1, 0.0, call)
-            put(ex_v, e + 2 + w, 0.05 if w else 0.4, v_re)
+            w = n // POW_COLS - 1
+            s_root, v_ndn, v_r, v_mid, s_q, v_end = chain(a, b)
+            root[e] = s_root
+            put(e, 1.0, v_ndn)
+            put(e + 1, 0.3, v_r[0])
+            put(e + 1, 0.7, v_r[1])
+            for i in range(w + 1):
+                gate[e + 1 + i] = powers(a + i * POW_COLS)
             for i, call in enumerate(v_mid):
-                put(ex_v, e + 2 + w, (0.15 if w else 0.5) + 0.06 * i, call)
-            put(ex_g, e + 2 + w, 0.0, g_x1)
-            put(ex_s, e + 3 + w, 0.15, s_q)
-            put(ex_v, e + 3 + w, 0.4, v_mx)
-            put(ex_v, e + 3 + w, 0.55, v_rf)
-            put(ex_g, e + 3 + w, 0.0, g_al)
+                put(e + 2 + w, 0.05 + 0.08 * i, call)
+            early_s[e + 3 + w] = s_q
+            for i, call in enumerate(v_end):
+                end_v.setdefault(e + 3 + w, []).append((0.4 * i, call))
             for c in range(a // CH, b // CH):
                 avail[c] = e + 4 + w
             a = b
@@ -381,13 +387,12 @@ def tile_hypequalizedlinear_t_kernel(tc, x, weight, bias, out):
                 rcp(run[:], un[:]),
             ]
         }
-        put(ex_s, 0, 0.3, act(th[:], un[:], ACT.Tanh))
-        put(ex_v, 0, 0.0, tt(kk[:], th[:], run[:], ALU.mult))
-        put(ex_v, 0, 0.0, ts(b_pos[:], u_f[:], kk[:], None, ALU.mult))
-        put(ex_s, 1, 0.3, act(junk_d[1][:], b_pos[:], ACT.Square, y2[:]))
-        put(ex_v, 2, 0.0, ts(y2p1[:], y2[:], 1.0, None, ALU.add))
+        early_s[0] = act(th[:], un[:], ACT.Tanh)
+        put(0, 0.0, tt(kk[:], th[:], run[:], ALU.mult))
+        put(0, 0.0, ts(b_pos[:], u_f[:], kk[:], None, ALU.mult))
+        early_s[1] = act(junk_d[1][:], b_pos[:], ACT.Square, y2[:])
+        put(2, 0.0, ts(y2p1[:], y2[:], 1.0, None, ALU.add))
 
-        pending = []
         for s in range(len(p2) - 1):
             if s % 2 == 0 and s // 2 + LOOKAHEAD < NCH // 2:
                 load(s // 2 + LOOKAHEAD, 1)
@@ -395,14 +400,35 @@ def tile_hypequalizedlinear_t_kernel(tc, x, weight, bias, out):
                 copies(s, len(p2[s]))
             for f in first_v.get(s, []):
                 f()
-            s_calls = []
-            v_squares = []
             if 0 <= s - 2 < NCH:
-                s_calls += m_squares(s - 2)
-            if s < NCH:
-                calls, v_squares = x_squares(s, 1 if not p2[s] and s % 2 == 1 else 0)
-                s_calls += calls
-            weave(s_calls, ex_s.get(s, []))
+                for f in m_dot_b(s - 2):
+                    f()
+            relus = []
+            for c in p2[s]:
+                calls, last = finish(c)
+                for f in calls:
+                    f()
+                relus += last
+
+            squares, v_squares = x_squares(s, 1 if not p2[s] and s % 2 == 1 else 0) if s < NCH else ([], [])
+            for i, f in enumerate(squares):
+                f()
+                if i == 0 and s in early_s:
+                    early_s[s]()
+                if i == 1 and 0 <= s - 2 < NCH:
+                    for h in m_squares(s - 2):
+                        h()
+                    if s in root:
+                        root[s]()
+            if s >= NCH:
+                if s in early_s:
+                    early_s[s]()
+                if s - 2 < NCH:
+                    for h in m_squares(s - 2):
+                        h()
+                if s in root:
+                    root[s]()
+
             if 0 <= s - 1 < NCH:
                 quantise(s - 1)
             if s + 1 < NCH:
@@ -410,18 +436,14 @@ def tile_hypequalizedlinear_t_kernel(tc, x, weight, bias, out):
             if 0 <= s - 1 < NCH:
                 products(s - 1, ps_ms, "ms", ms_of)
                 products(s - 1, ps_mv, "mv", mv_of)
-            v_calls = v_squares
-            dots = m_dot_b(s - 2) if 0 <= s - 2 < NCH else []
-            for c in p2[s]:
-                calls, last = finish(c)
-                v_calls += pending + dots + calls
-                pending = last
-                dots = []
-            v_calls += dots
-            if s == len(p2) - 2:
-                v_calls += pending
-            weave(v_calls, ex_v.get(s, []))
-            weave([], ex_g.get(s, []))
+            terms = []
             for c in p2[s + 1]:
-                bias_terms(c)
+                terms += bias_terms(c)
+            weave(relus + v_squares, end_v.get(s, []))
+            weave(terms, ex_v.get(s, []))
+            if s in gate:
+                v_base, g_power = gate[s]
+                v_base()
+                g_power()
+            for c in p2[s + 1]:
                 products(c, ps_m2, "m2", m2_of)

@@ -65,6 +65,7 @@ def tile_hypequalizedlinear_t_kernel(tc, x, weight, bias, out):
         w_scales = const.tile([P, DOUT], U8, name="w_scales", align_bytes=64)
         u_f = const.tile([P, DOUT], F32, name="u_f")
         b_pos = const.tile([P, DOUT], F32, name="b_pos")
+        b_neg = const.tile([P, DOUT], F32, name="b_neg")
         un2 = col("un2")
         un2c = col("un2c")
         un = col("un")
@@ -88,7 +89,7 @@ def tile_hypequalizedlinear_t_kernel(tc, x, weight, bias, out):
         c_t = wide("c_t")
         c_s = wide("c_s")
         c_x2 = wide("c_x2")
-        c_x1 = wide("c_x1")
+        nbe = wide("nbe")
         c_xy = wide("c_xy")
         c_d0 = wide("c_d0")
         c_den = wide("c_den")
@@ -125,19 +126,21 @@ def tile_hypequalizedlinear_t_kernel(tc, x, weight, bias, out):
         def act(o, i, func, acc=None, add=0.0):
             return lambda: sc.activation(out=o, in_=i, func=func, bias=add, accum_out=acc)
 
+        def scaled(o, i, s):
+            return lambda: sc.activation(out=o, in_=i, func=ACT.Copy, scale=s)
+
         def gtt(o, i0, i1, op):
             return lambda: g_.tensor_tensor(out=o, in0=i0, in1=i1, op=op)
 
         def weave(bulk, extras):
-            order = sorted(extras, key=lambda e: e[0])
-            i = 0
+            done = 0
             for n, f in enumerate(bulk):
-                while i < len(order) and order[i][0] * len(bulk) <= n:
-                    order[i][1]()
-                    i += 1
                 f()
-            for e in order[i:]:
-                e[1]()
+                while done < len(extras) and (done + 1) * len(bulk) <= (n + 1) * len(extras):
+                    extras[done]()
+                    done += 1
+            for f in extras[done:]:
+                f()
 
         def mx(dst, t):
             nc.tensor.matmul_mx(
@@ -176,13 +179,15 @@ def tile_hypequalizedlinear_t_kernel(tc, x, weight, bias, out):
             g = gpool.tile([P, CH * K], BF16, name="g", align_bytes=64)
             g_of[c] = g
             gw = g[:].bitcast(F32)
+            calls = []
             for h in range(2):
                 dst = gw[:, h * 512 : (h + 1) * 512].rearrange("p (t r u) -> p t r u", t=2, u=2)
                 src = xt_of[c][h][:].rearrange("p (t u r) -> p t r u", t=2, u=2)
                 if h >= 2 - on_scalar:
                     sc.copy(out=dst, in_=src)
                 else:
-                    v.tensor_copy(out=dst, in_=src)
+                    calls.append(lambda dst=dst, src=src: v.tensor_copy(out=dst, in_=src))
+            return calls
 
         def x_squares(c, n_v):
             xs = xs_of[c // 2]
@@ -239,15 +244,17 @@ def tile_hypequalizedlinear_t_kernel(tc, x, weight, bias, out):
                 in_=y_of[c // 2][:].rearrange("p (t o) -> p t o", o=DOUT),
             )
 
-        def bias_terms(c):
+        def bias_terms(c, on_scalar):
             bb = bpool.tile([P, CH * DOUT], F32, name="bb")
             bb_of[c] = bb
             calls = []
             for j in range(CH):
                 t = c * CH + j
-                calls.append(
-                    ts(bb[:, j * P : (j + 1) * P], b_pos[:], c_x1[:, t : t + 1], c_rf[:, t : t + 1], ALU.mult, ALU.mult)
-                )
+                dst = bb[:, j * P : (j + 1) * P]
+                if on_scalar:
+                    calls.append(scaled(dst, b_neg[:], nbe[:, t : t + 1]))
+                else:
+                    calls.append(ts(dst, b_neg[:], nbe[:, t : t + 1], None, ALU.mult))
             return calls
 
         def finish(c):
@@ -286,8 +293,8 @@ def tile_hypequalizedlinear_t_kernel(tc, x, weight, bias, out):
             rxn = c_rnrm[:, 0, sl]
             rmn = c_rnrm[:, 1, sl]
             s_root = act(c_nrm[:, 0:2, sl], s2[:, :, sl], ACT.Sqrt, add=1e-30)
-            v_ndn = ts(c_nrm[:, 2, sl], c_nrm[:, 0, sl], 1.0 - 1e-5, 1.0, ALU.min, ALU.subtract)
             v_r = [
+                ts(c_nrm[:, 2, sl], c_nrm[:, 0, sl], 1.0 - 1e-5, 1.0, ALU.min, ALU.subtract),
                 rcp(c_rnrm[:, :, sl], c_nrm[:, :, sl]),
                 tt(c_r[:, sl], c_nrm[:, 1, sl], rxn, ALU.mult),
             ]
@@ -298,7 +305,8 @@ def tile_hypequalizedlinear_t_kernel(tc, x, weight, bias, out):
                 tt(c_s[:, sl], c_t[:, sl], rmn, ALU.mult),
                 tt(c_x2[:, sl], c_t[:, sl], c_t[:, sl], ALU.mult),
                 tt(c_xy[:, sl], c_s[:, sl], pb[:, sl], ALU.mult),
-                ts(c_x1[:, sl], c_x2[:, sl], -1.0, 1.0, ALU.mult, ALU.add),
+            ]
+            v_den = [
                 stt(c_d0[:, sl], c_x2[:, sl], y2[:], c_xy[:, sl], ALU.mult, ALU.add),
                 stt(c_num[:, sl], c_x2[:, sl], y2[:], c_xy[:, sl], ALU.add, ALU.add),
                 ts(c_den[:, sl], c_d0[:, sl], 1.0, 1e-15, ALU.add, ALU.max),
@@ -312,39 +320,36 @@ def tile_hypequalizedlinear_t_kernel(tc, x, weight, bias, out):
             v_end = [
                 tt(c_mx[:, sl], c_den[:, sl], c_q[:, sl], ALU.max),
                 rcp(c_rf[:, sl], c_mx[:, sl]),
+                stt(nbe[:, sl], c_x2[:, sl], 1.0, c_rf[:, sl], ALU.subtract, ALU.mult),
                 tt(al[:, sl], c_as[:, sl], c_rf[:, sl], ALU.mult),
             ]
-            return s_root, v_ndn, v_r, v_mid, s_q, v_end
+            return s_root, v_r, v_mid, v_den, s_q, v_end
 
-        ex_v = {}
-        end_v = {}
+        half1 = {}
+        half2 = {}
+        ends = {}
         gate = {}
         root = {}
         early_s = {}
-
-        def put(s, f, call):
-            ex_v.setdefault(s, []).append((f, call))
+        late_s = {}
 
         avail = [0] * NCH
         a = 0
         for n in GROUPS:
             b = a + n
             e = b // CH + 1
-            w = n // POW_COLS - 1
-            s_root, v_ndn, v_r, v_mid, s_q, v_end = chain(a, b)
-            root[e] = s_root
-            put(e, 1.0, v_ndn)
-            put(e + 1, 0.3, v_r[0])
-            put(e + 1, 0.7, v_r[1])
-            for i in range(w + 1):
+            w = n // POW_COLS
+            s_root, v_r, v_mid, v_den, s_q, v_end = chain(a, b)
+            root[e] = [s_root]
+            half1[e + 1] = half1.get(e + 1, []) + v_r
+            for i in range(w):
                 gate[e + 1 + i] = powers(a + i * POW_COLS)
-            for i, call in enumerate(v_mid):
-                put(e + 2 + w, 0.05 + 0.08 * i, call)
-            early_s[e + 3 + w] = s_q
-            for i, call in enumerate(v_end):
-                end_v.setdefault(e + 3 + w, []).append((0.4 * i, call))
+            half2[e + 1 + w] = half2.get(e + 1 + w, []) + v_mid
+            half1[e + 2 + w] = half1.get(e + 2 + w, []) + v_den
+            late_s[e + 2 + w] = [s_q]
+            ends[e + 2 + w] = v_end
             for c in range(a // CH, b // CH):
-                avail[c] = e + 4 + w
+                avail[c] = e + 3 + w
             a = b
         p2 = []
         done = 0
@@ -387,48 +392,42 @@ def tile_hypequalizedlinear_t_kernel(tc, x, weight, bias, out):
                 rcp(run[:], un[:]),
             ]
         }
-        early_s[0] = act(th[:], un[:], ACT.Tanh)
-        put(0, 0.0, tt(kk[:], th[:], run[:], ALU.mult))
-        put(0, 0.0, ts(b_pos[:], u_f[:], kk[:], None, ALU.mult))
-        early_s[1] = act(junk_d[1][:], b_pos[:], ACT.Square, y2[:])
-        put(2, 0.0, ts(y2p1[:], y2[:], 1.0, None, ALU.add))
+        early_s[0] = [act(th[:], un[:], ACT.Tanh)]
+        half2[0] = [
+            tt(kk[:], th[:], run[:], ALU.mult),
+            ts(b_pos[:], u_f[:], kk[:], None, ALU.mult),
+            ts(b_neg[:], u_f[:], kk[:], -1.0, ALU.mult, ALU.mult),
+        ]
+        early_s[1] = [act(junk_d[1][:], b_pos[:], ACT.Square, y2[:])]
+        half2[2] = [ts(y2p1[:], y2[:], 1.0, None, ALU.add)]
 
         for s in range(len(p2) - 1):
+            bulk = s < NCH
             if s % 2 == 0 and s // 2 + LOOKAHEAD < NCH // 2:
                 load(s // 2 + LOOKAHEAD, 1)
-            if s < NCH:
-                copies(s, len(p2[s]))
-            for f in first_v.get(s, []):
-                f()
-            if 0 <= s - 2 < NCH:
-                for f in m_dot_b(s - 2):
+            first = copies(s, (1 + s % 2) if p2[s] else 0) if bulk else []
+            if s in first_v:
+                for f in first + first_v[s]:
                     f()
+                first = []
+            if 0 <= s - 2 < NCH:
+                first += m_dot_b(s - 2)
             relus = []
             for c in p2[s]:
                 calls, last = finish(c)
-                for f in calls:
-                    f()
+                first += calls
                 relus += last
+            weave(first, half1.get(s, []))
 
-            squares, v_squares = x_squares(s, 1 if not p2[s] and s % 2 == 1 else 0) if s < NCH else ([], [])
-            for i, f in enumerate(squares):
+            squares, v_squares = x_squares(s, 1 if not p2[s] and s % 2 == 1 else 0) if bulk else ([], [])
+            sums = m_squares(s - 2) if 0 <= s - 2 < NCH else []
+            s_calls = squares[:1] + early_s.get(s, []) + squares[1:2] + sums + root.get(s, [])
+            for f in s_calls + squares[2:3] + late_s.get(s, []) + squares[3:]:
                 f()
-                if i == 0 and s in early_s:
-                    early_s[s]()
-                if i == 1 and 0 <= s - 2 < NCH:
-                    for h in m_squares(s - 2):
-                        h()
-                    if s in root:
-                        root[s]()
-            if s >= NCH:
-                if s in early_s:
-                    early_s[s]()
-                if s - 2 < NCH:
-                    for h in m_squares(s - 2):
-                        h()
-                if s in root:
-                    root[s]()
 
+            last_calls = ends.get(s, [])
+            for f in last_calls[:1]:
+                f()
             if 0 <= s - 1 < NCH:
                 quantise(s - 1)
             if s + 1 < NCH:
@@ -436,11 +435,14 @@ def tile_hypequalizedlinear_t_kernel(tc, x, weight, bias, out):
             if 0 <= s - 1 < NCH:
                 products(s - 1, ps_ms, "ms", ms_of)
                 products(s - 1, ps_mv, "mv", mv_of)
+            for f in last_calls[1:2] + relus[:1] + last_calls[2:]:
+                f()
             terms = []
             for c in p2[s + 1]:
-                terms += bias_terms(c)
-            weave(relus + v_squares, end_v.get(s, []))
-            weave(terms, ex_v.get(s, []))
+                terms += bias_terms(c, not bulk)
+            weave(relus[1:] + v_squares + (terms if bulk else []), half2.get(s, []))
+            if not bulk:
+                weave(terms, [])
             if s in gate:
                 v_base, g_power = gate[s]
                 v_base()

@@ -34,9 +34,8 @@ def tile_hypequalizedlinear_t_kernel(tc, x, weight, bias, out):
         gpool = ctx.enter_context(tc.tile_pool(name="gpool", bufs=3))
         bpool = ctx.enter_context(tc.tile_pool(name="bpool", bufs=4))
         ypool = ctx.enter_context(tc.tile_pool(name="ypool", bufs=4))
-        ps_xt = ctx.enter_context(tc.psum_pool(name="ps_xt", bufs=2))
-        ps_ms = ctx.enter_context(tc.psum_pool(name="ps_ms", bufs=2))
-        ps_mv = ctx.enter_context(tc.psum_pool(name="ps_mv", bufs=2))
+        ps_xt = ctx.enter_context(tc.psum_pool(name="ps_xt", bufs=3))
+        ps_mm = ctx.enter_context(tc.psum_pool(name="ps_mm", bufs=3))
         ps_m2 = ctx.enter_context(tc.psum_pool(name="ps_m2", bufs=2))
 
         ctx.enter_context(tc.manual_schedule())
@@ -103,8 +102,7 @@ def tile_hypequalizedlinear_t_kernel(tc, x, weight, bias, out):
         xs_of = {}
         xt_of = {}
         g_of = {}
-        ms_of = {}
-        mv_of = {}
+        mm_of = {}
         m2_of = {}
         bb_of = {}
         y_of = {}
@@ -220,7 +218,7 @@ def tile_hypequalizedlinear_t_kernel(tc, x, weight, bias, out):
 
         def m_squares(c):
             return [
-                act(junk_d[j][:], ms_of[c][:, j * P : (j + 1) * P], ACT.Square, s2[:, 1, c * CH + j : c * CH + j + 1])
+                act(junk_d[j][:], mm_of[c][:, j * P : (j + 1) * P], ACT.Square, s2[:, 1, c * CH + j : c * CH + j + 1])
                 for j in range(CH)
             ]
 
@@ -228,7 +226,7 @@ def tile_hypequalizedlinear_t_kernel(tc, x, weight, bias, out):
             return [
                 stt(
                     junk_e[j][:],
-                    mv_of[c][:, j * P : (j + 1) * P],
+                    mm_of[c][:, j * P : (j + 1) * P],
                     2.0,
                     b_pos[:],
                     ALU.mult,
@@ -337,13 +335,13 @@ def tile_hypequalizedlinear_t_kernel(tc, x, weight, bias, out):
         a = 0
         for n in GROUPS:
             b = a + n
-            e = b // CH + 1
+            e = b // CH
             w = n // POW_COLS
             s_root, v_r, v_mid, v_den, s_q, v_end = chain(a, b)
             root[e] = [s_root]
             half1[e + 1] = half1.get(e + 1, []) + v_r
             for i in range(w):
-                gate[e + 1 + i] = powers(a + i * POW_COLS)
+                gate[e + 2 + i] = powers(a + i * POW_COLS)
             half2[e + 1 + w] = half2.get(e + 1 + w, []) + v_mid
             half1[e + 2 + w] = half1.get(e + 2 + w, []) + v_den
             late_s[e + 2 + w] = [s_q]
@@ -371,7 +369,7 @@ def tile_hypequalizedlinear_t_kernel(tc, x, weight, bias, out):
         for blk in range(1, LOOKAHEAD):
             load(blk, 1)
         transposes(0)
-        w_bank = ps_ms.tile([P, 512], F32, name="ms")
+        w_bank = ps_mm.tile([P, 512], F32, name="mm")
         w_words = w_raw[:].bitcast(F32)
         for u in range(2):
             nc.tensor.transpose(w_bank[:, u * P : (u + 1) * P], w_words[:, u : K // 2 : 2], ident[:])
@@ -405,6 +403,13 @@ def tile_hypequalizedlinear_t_kernel(tc, x, weight, bias, out):
             bulk = s < NCH
             if s % 2 == 0 and s // 2 + LOOKAHEAD < NCH // 2:
                 load(s // 2 + LOOKAHEAD, 1)
+            if 0 <= s - 1 < NCH:
+                quantise(s - 1)
+                products(s - 1, ps_mm, "mm", mm_of)
+            if s in gate:
+                v_base, g_power = gate[s]
+                v_base()
+                g_power()
             first = copies(s, (1 + s % 2) if p2[s] else 0) if bulk else []
             if s in first_v:
                 for f in first + first_v[s]:
@@ -418,34 +423,23 @@ def tile_hypequalizedlinear_t_kernel(tc, x, weight, bias, out):
                 first += calls
                 relus += last
             weave(first, half1.get(s, []))
+            if s + 1 < NCH:
+                transposes(s + 1)
 
             squares, v_squares = x_squares(s, 1 if not p2[s] and s % 2 == 1 else 0) if bulk else ([], [])
-            sums = m_squares(s - 2) if 0 <= s - 2 < NCH else []
-            s_calls = squares[:1] + early_s.get(s, []) + squares[1:2] + sums + root.get(s, [])
-            for f in s_calls + squares[2:3] + late_s.get(s, []) + squares[3:]:
+            sums = m_squares(s - 1) if 0 <= s - 1 < NCH else []
+            s_calls = squares[:1] + early_s.get(s, []) + squares[1:2] + late_s.get(s, []) + squares[2:3]
+            for f in s_calls + sums + root.get(s, []) + squares[3:]:
                 f()
 
             last_calls = ends.get(s, [])
-            for f in last_calls[:1]:
-                f()
-            if 0 <= s - 1 < NCH:
-                quantise(s - 1)
-            if s + 1 < NCH:
-                transposes(s + 1)
-            if 0 <= s - 1 < NCH:
-                products(s - 1, ps_ms, "ms", ms_of)
-                products(s - 1, ps_mv, "mv", mv_of)
-            for f in last_calls[1:2] + relus[:1] + last_calls[2:]:
+            for f in last_calls[:1] + relus[:1] + last_calls[1:2] + relus[1:] + last_calls[2:]:
                 f()
             terms = []
             for c in p2[s + 1]:
                 terms += bias_terms(c, not bulk)
-            weave(relus[1:] + v_squares + (terms if bulk else []), half2.get(s, []))
+            weave(v_squares + (terms if bulk else []), half2.get(s, []))
             if not bulk:
                 weave(terms, [])
-            if s in gate:
-                v_base, g_power = gate[s]
-                v_base()
-                g_power()
             for c in p2[s + 1]:
                 products(c, ps_m2, "m2", m2_of)

@@ -34,8 +34,8 @@ def tile_hypequalizedlinear_t_kernel(tc, x, weight, bias, out):
         gpool = ctx.enter_context(tc.tile_pool(name="gpool", bufs=3))
         bpool = ctx.enter_context(tc.tile_pool(name="bpool", bufs=4))
         ypool = ctx.enter_context(tc.tile_pool(name="ypool", bufs=4))
-        ps_xt = ctx.enter_context(tc.psum_pool(name="ps_xt", bufs=3))
-        ps_mm = ctx.enter_context(tc.psum_pool(name="ps_mm", bufs=3))
+        ps_xt = ctx.enter_context(tc.psum_pool(name="ps_xt", bufs=2))
+        ps_mm = ctx.enter_context(tc.psum_pool(name="ps_mm", bufs=4))
         ps_m2 = ctx.enter_context(tc.psum_pool(name="ps_m2", bufs=2))
 
         ctx.enter_context(tc.manual_schedule())
@@ -335,19 +335,19 @@ def tile_hypequalizedlinear_t_kernel(tc, x, weight, bias, out):
         a = 0
         for n in GROUPS:
             b = a + n
-            e = b // CH
+            e = b // CH + 1
             w = n // POW_COLS
             s_root, v_r, v_mid, v_den, s_q, v_end = chain(a, b)
             root[e] = [s_root]
             half1[e + 1] = half1.get(e + 1, []) + v_r
             for i in range(w):
                 gate[e + 2 + i] = powers(a + i * POW_COLS)
-            half2[e + 1 + w] = half2.get(e + 1 + w, []) + v_mid
-            half1[e + 2 + w] = half1.get(e + 2 + w, []) + v_den
+            half2[e + 1 + w] = half2.get(e + 1 + w, []) + v_mid[:3]
+            half1[e + 2 + w] = half1.get(e + 2 + w, []) + v_mid[3:] + v_den
             late_s[e + 2 + w] = [s_q]
-            ends[e + 2 + w] = v_end
+            ends[e + 3 + w] = v_end
             for c in range(a // CH, b // CH):
-                avail[c] = e + 3 + w
+                avail[c] = e + 4 + w
             a = b
         p2 = []
         done = 0
@@ -397,12 +397,14 @@ def tile_hypequalizedlinear_t_kernel(tc, x, weight, bias, out):
             ts(b_neg[:], u_f[:], kk[:], -1.0, ALU.mult, ALU.mult),
         ]
         early_s[1] = [act(junk_d[1][:], b_pos[:], ACT.Square, y2[:])]
-        half2[2] = [ts(y2p1[:], y2[:], 1.0, None, ALU.add)]
+        half2[3] = [ts(y2p1[:], y2[:], 1.0, None, ALU.add)]
 
         for s in range(len(p2) - 1):
             bulk = s < NCH
             if s % 2 == 0 and s // 2 + LOOKAHEAD < NCH // 2:
                 load(s // 2 + LOOKAHEAD, 1)
+            for f in ends.get(s, [])[:1]:
+                f()
             if 0 <= s - 1 < NCH:
                 quantise(s - 1)
                 products(s - 1, ps_mm, "mm", mm_of)
@@ -415,30 +417,27 @@ def tile_hypequalizedlinear_t_kernel(tc, x, weight, bias, out):
                 for f in first + first_v[s]:
                     f()
                 first = []
-            if 0 <= s - 2 < NCH:
-                first += m_dot_b(s - 2)
             relus = []
             for c in p2[s]:
                 calls, last = finish(c)
                 first += calls
                 relus += last
-            weave(first, half1.get(s, []))
+            if 0 <= s - 3 < NCH:
+                first += m_dot_b(s - 3)
+            weave(first, ends.get(s, [])[1:] + half1.get(s, []))
             if s + 1 < NCH:
                 transposes(s + 1)
 
             squares, v_squares = x_squares(s, 1 if not p2[s] and s % 2 == 1 else 0) if bulk else ([], [])
-            sums = m_squares(s - 1) if 0 <= s - 1 < NCH else []
-            s_calls = squares[:1] + early_s.get(s, []) + squares[1:2] + late_s.get(s, []) + squares[2:3]
-            for f in s_calls + sums + root.get(s, []) + squares[3:]:
+            sums = m_squares(s - 2) if 0 <= s - 2 < NCH else []
+            s_calls = squares[:1] + early_s.get(s, []) + squares[1:3] + sums + root.get(s, []) + squares[3:]
+            for f in s_calls + late_s.get(s, []):
                 f()
 
-            last_calls = ends.get(s, [])
-            for f in last_calls[:1] + relus[:1] + last_calls[1:2] + relus[1:] + last_calls[2:]:
-                f()
             terms = []
             for c in p2[s + 1]:
                 terms += bias_terms(c, not bulk)
-            weave(v_squares + (terms if bulk else []), half2.get(s, []))
+            weave(relus + v_squares + (terms if bulk else []), half2.get(s, []))
             if not bulk:
                 weave(terms, [])
             for c in p2[s + 1]:

@@ -325,7 +325,6 @@ def tile_hypequalizedlinear_t_kernel(tc, x, weight, bias, out):
 
         half1 = {}
         half2 = {}
-        ends = {}
         gate = {}
         root = {}
         early_s = {}
@@ -345,7 +344,7 @@ def tile_hypequalizedlinear_t_kernel(tc, x, weight, bias, out):
             half2[e + 1 + w] = half2.get(e + 1 + w, []) + v_mid[:3]
             half1[e + 2 + w] = half1.get(e + 2 + w, []) + v_mid[3:] + v_den
             late_s[e + 2 + w] = [s_q]
-            ends[e + 3 + w] = v_end
+            half1[e + 3 + w] = half1.get(e + 3 + w, []) + v_end
             for c in range(a // CH, b // CH):
                 avail[c] = e + 4 + w
             a = b
@@ -364,7 +363,7 @@ def tile_hypequalizedlinear_t_kernel(tc, x, weight, bias, out):
         make_identity(nc, ident[:])
         v.memset(half[:], 0.5)
         sc.dma_start(out=bias_bc[:], in_=bias.partition_broadcast(P))
-        load(0, 2)
+        load(0, 4)
         nc.sync.dma_start(out=w_raw[:], in_=weight)
         for blk in range(1, LOOKAHEAD):
             load(blk, 1)
@@ -390,21 +389,19 @@ def tile_hypequalizedlinear_t_kernel(tc, x, weight, bias, out):
                 rcp(run[:], un[:]),
             ]
         }
-        early_s[0] = [act(th[:], un[:], ACT.Tanh)]
-        half2[0] = [
+        early_s[1] = [act(th[:], un[:], ACT.Tanh)]
+        half2[1] = [
             tt(kk[:], th[:], run[:], ALU.mult),
             ts(b_pos[:], u_f[:], kk[:], None, ALU.mult),
             ts(b_neg[:], u_f[:], kk[:], -1.0, ALU.mult, ALU.mult),
         ]
-        early_s[1] = [act(junk_d[1][:], b_pos[:], ACT.Square, y2[:])]
+        early_s[2] = [act(junk_d[1][:], b_pos[:], ACT.Square, y2[:])]
         half2[3] = [ts(y2p1[:], y2[:], 1.0, None, ALU.add)]
 
         for s in range(len(p2) - 1):
             bulk = s < NCH
             if s % 2 == 0 and s // 2 + LOOKAHEAD < NCH // 2:
                 load(s // 2 + LOOKAHEAD, 1)
-            for f in ends.get(s, [])[:1]:
-                f()
             if 0 <= s - 1 < NCH:
                 quantise(s - 1)
                 products(s - 1, ps_mm, "mm", mm_of)
@@ -412,7 +409,7 @@ def tile_hypequalizedlinear_t_kernel(tc, x, weight, bias, out):
                 v_base, g_power = gate[s]
                 v_base()
                 g_power()
-            first = copies(s, (1 + s % 2) if p2[s] else 0) if bulk else []
+            first = copies(s, 1 if p2[s] else 0) if bulk else []
             if s in first_v:
                 for f in first + first_v[s]:
                     f()
@@ -424,7 +421,7 @@ def tile_hypequalizedlinear_t_kernel(tc, x, weight, bias, out):
                 relus += last
             if 0 <= s - 3 < NCH:
                 first += m_dot_b(s - 3)
-            weave(first, ends.get(s, [])[1:] + half1.get(s, []))
+            weave(first, half1.get(s, []))
             if s + 1 < NCH:
                 transposes(s + 1)
 

@@ -19,8 +19,11 @@ DOUT = 128
 NT = 128
 CH = 4
 NCH = NT // CH
-GROUPS = (16, 16, 16, 16, 16, 16, 16, 8, 8)
+GROUP = 16
+LAG = 11
 POW_COLS = 8
+G_ON_S = 1
+N_ON_S = 2
 LOOKAHEAD = 4
 
 
@@ -286,21 +289,23 @@ def tile_hypequalizedlinear_t_kernel(tc, x, weight, bias, out):
                 gtt(c_e[:, sl], c_base[:, sl], c_r[:, sl], ALU.pow),
             )
 
-        def chain(a, b):
+        def front(a, b):
             sl = slice(a, b)
-            rxn = c_rnrm[:, 0, sl]
-            rmn = c_rnrm[:, 1, sl]
             s_root = act(c_nrm[:, 0:2, sl], s2[:, :, sl], ACT.Sqrt, add=1e-30)
             v_r = [
                 ts(c_nrm[:, 2, sl], c_nrm[:, 0, sl], 1.0 - 1e-5, 1.0, ALU.min, ALU.subtract),
                 rcp(c_rnrm[:, :, sl], c_nrm[:, :, sl]),
-                tt(c_r[:, sl], c_nrm[:, 1, sl], rxn, ALU.mult),
+                tt(c_r[:, sl], c_nrm[:, 1, sl], c_rnrm[:, 0, sl], ALU.mult),
             ]
+            return s_root, v_r
+
+        def back(a, b):
+            sl = slice(a, b)
             v_mid = [
                 ts(c_e1[:, sl], c_e[:, sl], 1.0, None, ALU.add),
                 rcp(c_re[:, sl], c_e1[:, sl]),
                 ts(c_t[:, sl], c_re[:, sl], -2.0, 1.0, ALU.mult, ALU.add),
-                tt(c_s[:, sl], c_t[:, sl], rmn, ALU.mult),
+                tt(c_s[:, sl], c_t[:, sl], c_rnrm[:, 1, sl], ALU.mult),
                 tt(c_x2[:, sl], c_t[:, sl], c_t[:, sl], ALU.mult),
                 tt(c_xy[:, sl], c_s[:, sl], pb[:, sl], ALU.mult),
             ]
@@ -321,44 +326,27 @@ def tile_hypequalizedlinear_t_kernel(tc, x, weight, bias, out):
                 stt(nbe[:, sl], c_x2[:, sl], 1.0, c_rf[:, sl], ALU.subtract, ALU.mult),
                 tt(al[:, sl], c_as[:, sl], c_rf[:, sl], ALU.mult),
             ]
-            return s_root, v_r, v_mid, v_den, s_q, v_end
+            return v_mid, v_den, s_q, v_end
 
         half1 = {}
         half2 = {}
         gate = {}
         root = {}
+        first_s = {}
         early_s = {}
-        late_s = {}
 
-        avail = [0] * NCH
-        a = 0
-        for n in GROUPS:
-            b = a + n
+        for b in range(GROUP, NT, GROUP):
+            a = b - GROUP
             e = b // CH + 1
-            w = n // POW_COLS
-            s_root, v_r, v_mid, v_den, s_q, v_end = chain(a, b)
+            s_root, v_r = front(a, b)
+            v_mid, v_den, s_q, v_end = back(a, b)
             root[e] = [s_root]
-            half1[e + 1] = half1.get(e + 1, []) + v_r
-            for i in range(w):
-                gate[e + 2 + i] = powers(a + i * POW_COLS)
-            half2[e + 1 + w] = half2.get(e + 1 + w, []) + v_mid[:3]
-            half1[e + 2 + w] = half1.get(e + 2 + w, []) + v_mid[3:] + v_den
-            late_s[e + 2 + w] = [s_q]
-            half1[e + 3 + w] = half1.get(e + 3 + w, []) + v_end
-            for c in range(a // CH, b // CH):
-                avail[c] = e + 4 + w
-            a = b
-        p2 = []
-        done = 0
-        while done < NCH:
-            s = len(p2)
-            cap = 1 if s < NCH else 2
-            now = []
-            while len(now) < cap and done < NCH and avail[done] <= s:
-                now.append(done)
-                done += 1
-            p2.append(now)
-        p2.append([])
+            half1[e + 1] = v_r + half1.get(e + 1, [])
+            gate[e + 2] = powers(a)
+            gate[e + 3] = powers(a + POW_COLS)
+            half1[e + 4] = half1.get(e + 4, []) + v_mid + v_den
+            first_s[e + 5] = [s_q]
+            half1[e + 5] = half1.get(e + 5, []) + v_end
 
         make_identity(nc, ident[:])
         v.memset(half[:], 0.5)
@@ -398,44 +386,109 @@ def tile_hypequalizedlinear_t_kernel(tc, x, weight, bias, out):
         early_s[2] = [act(junk_d[1][:], b_pos[:], ACT.Square, y2[:])]
         half2[3] = [ts(y2p1[:], y2[:], 1.0, None, ALU.add)]
 
-        for s in range(len(p2) - 1):
-            bulk = s < NCH
+        dots = []
+        for s in range(NCH):
+            fin = s >= LAG
             if s % 2 == 0 and s // 2 + LOOKAHEAD < NCH // 2:
                 load(s // 2 + LOOKAHEAD, 1)
-            if 0 <= s - 1 < NCH:
+            if s in gate:
+                gate[s][0]()
+            if s >= 1:
                 quantise(s - 1)
                 products(s - 1, ps_mm, "mm", mm_of)
             if s in gate:
-                v_base, g_power = gate[s]
-                v_base()
-                g_power()
-            first = copies(s, 1 if p2[s] else 0) if bulk else []
+                gate[s][1]()
+            for f in first_s.get(s, []):
+                f()
+            first = copies(s, (G_ON_S if s in gate else N_ON_S) if fin else 0)
+            squares, v_squares = x_squares(s, 1 if s in (1, 3, 5) else 0)
+            for f in squares[:1] + early_s.get(s, []):
+                f()
             if s in first_v:
                 for f in first + first_v[s]:
                     f()
                 first = []
             relus = []
-            for c in p2[s]:
-                calls, last = finish(c)
+            if fin:
+                calls, relus = finish(s - LAG)
                 first += calls
-                relus += last
-            if 0 <= s - 3 < NCH:
-                first += m_dot_b(s - 3)
+            if s >= 3:
+                dots += m_dot_b(s - 3)
+            n_dots = (6 if s in gate else max(2, len(dots) - 4)) if s > 4 else len(dots)
+            first += dots[:n_dots]
+            dots = dots[n_dots:]
             weave(first, half1.get(s, []))
             if s + 1 < NCH:
                 transposes(s + 1)
 
-            squares, v_squares = x_squares(s, 1 if not p2[s] and s % 2 == 1 else 0) if bulk else ([], [])
-            sums = m_squares(s - 2) if 0 <= s - 2 < NCH else []
-            s_calls = squares[:1] + early_s.get(s, []) + squares[1:3] + sums + root.get(s, []) + squares[3:]
-            for f in s_calls + late_s.get(s, []):
+            sums = m_squares(s - 2) if s >= 2 else []
+            for f in squares[1:3] + sums + root.get(s, []) + squares[3:]:
+                f()
+            terms = bias_terms(s + 1 - LAG, False) if s + 1 >= LAG else []
+            weave(relus + v_squares + terms, half2.get(s, []))
+            if s + 1 >= LAG:
+                products(s + 1 - LAG, ps_m2, "m2", m2_of)
+
+        last = NT - GROUP
+        mid_p, den_p, q_p, end_p = back(last - GROUP, last)
+        mid_l, den_l, q_l, end_l = back(last, NT)
+        root_a, r_a = front(last, last + POW_COLS)
+        root_b, r_b = front(last + POW_COLS, NT)
+        base_p, power_p = gate[NCH]
+        base_a, power_a = powers(last)
+        base_b, power_b = powers(last + POW_COLS)
+        c0 = NCH - LAG
+        c_p = c0 + 3
+        c_l = c_p + 4
+
+        def do(*calls):
+            for f in calls:
                 f()
 
-            terms = []
-            for c in p2[s + 1]:
-                terms += bias_terms(c, not bulk)
-            weave(relus + v_squares + (terms if bulk else []), half2.get(s, []))
-            if not bulk:
-                weave(terms, [])
-            for c in p2[s + 1]:
-                products(c, ps_m2, "m2", m2_of)
+        base_p()
+        quantise(NCH - 1)
+        products(NCH - 1, ps_mm, "mm", mm_of)
+        power_p()
+        products(c0 + 1, ps_m2, "m2", m2_of)
+        do(*m_squares(NCH - 2), root_a)
+        do(*bias_terms(c0 + 1, True), *m_squares(NCH - 1), root_b)
+        do(*bias_terms(c0 + 2, True))
+        y0, relu0 = finish(c0)
+        y1, relu1 = finish(c0 + 1)
+        do(*dots, *y0, *m_dot_b(NCH - 3), *y1, *m_dot_b(NCH - 2))
+        products(c0 + 2, ps_m2, "m2", m2_of)
+        products(c_p, ps_xt, "xt", m2_of)
+        products(c_p + 1, ps_xt, "xt", m2_of)
+        y2_, relu2 = finish(c0 + 2)
+        weave(relu0 + relu1 + y2_, r_a + mid_p + den_p)
+        q_p()
+        weave(relu2, end_p)
+        base_a()
+        power_a()
+        for c in range(c_p, c_l):
+            do(*bias_terms(c, True))
+        do(*m_dot_b(NCH - 1))
+        products(c_p + 2, ps_m2, "m2", m2_of)
+        products(c_p + 3, ps_m2, "m2", m2_of)
+        y3, relu3 = finish(c_p)
+        y4, relu4 = finish(c_p + 1)
+        do(*y3, *y4)
+        weave(relu3 + relu4, r_b)
+        base_b()
+        power_b()
+        y5, relu5 = finish(c_p + 2)
+        y6, relu6 = finish(c_p + 3)
+        do(*y5, *y6)
+        for c in range(c_l, c_l + 2):
+            products(c, ps_xt, "xt", m2_of)
+        for c in range(c_l + 2, NCH):
+            products(c, ps_m2, "m2", m2_of)
+        weave(relu5, mid_l + den_l)
+        q_l()
+        weave(relu6, end_l)
+        do(*bias_terms(c_l, False))
+        for c in range(c_l + 1, NCH):
+            do(*bias_terms(c, True))
+        for c in range(c_l, NCH):
+            yc, reluc = finish(c)
+            do(*yc, *reluc)

@@ -20,10 +20,8 @@ NT = 128
 CH = 4
 NCH = NT // CH
 GROUP = 16
-LAG = 11
-POW_COLS = 8
-G_ON_S = 1
-N_ON_S = 2
+LAG = 9
+XV = (1, 3, 5)
 LOOKAHEAD = 4
 
 
@@ -258,7 +256,15 @@ def tile_hypequalizedlinear_t_kernel(tc, x, weight, bias, out):
                     calls.append(ts(dst, b_neg[:], nbe[:, t : t + 1], None, ALU.mult))
             return calls
 
-        def finish(c):
+        def scaled_products(c):
+            bb = bpool.tile([P, CH * DOUT], F32, name="bb")
+            bb_of[c] = bb
+            return [
+                scaled(bb[:, j * P : (j + 1) * P], m2_of[c][:, j * P : (j + 1) * P], al[:, c * CH + j : c * CH + j + 1])
+                for j in range(CH)
+            ]
+
+        def finish(c, is_scaled=False):
             if c % 2 == 0:
                 y_of[c // 2] = ypool.tile([P, 2 * CH * DOUT], F32, name="y")
             y = y_of[c // 2]
@@ -266,24 +272,20 @@ def tile_hypequalizedlinear_t_kernel(tc, x, weight, bias, out):
             calls = []
             for j in range(CH):
                 t = c * CH + j
-                calls.append(
-                    stt(
-                        y[:, off + j * P : off + (j + 1) * P],
-                        m2_of[c][:, j * P : (j + 1) * P],
-                        al[:, t : t + 1],
-                        bb_of[c][:, j * P : (j + 1) * P],
-                        ALU.mult,
-                        ALU.add,
-                    )
-                )
+                ysl = y[:, off + j * P : off + (j + 1) * P]
+                term = bb_of[c][:, j * P : (j + 1) * P]
+                if is_scaled:
+                    calls.append(stt(ysl, b_neg[:], nbe[:, t : t + 1], term, ALU.mult, ALU.add))
+                else:
+                    calls.append(stt(ysl, m2_of[c][:, j * P : (j + 1) * P], al[:, t : t + 1], term, ALU.mult, ALU.add))
             ysl = y[:, off : off + CH * DOUT]
             last = [stt(ysl, ysl, 0.2, ysl, ALU.mult, ALU.max)]
             if c % 2 == 1:
                 last.append(store(c))
             return calls, last
 
-        def powers(i):
-            sl = slice(i, i + POW_COLS)
+        def powers(a, b):
+            sl = slice(a, b)
             return (
                 ts(c_base[:, sl], c_rnrm[:, 2, sl], -2.0, -1.0, ALU.mult, ALU.add),
                 gtt(c_e[:, sl], c_base[:, sl], c_r[:, sl], ALU.pow),
@@ -341,12 +343,11 @@ def tile_hypequalizedlinear_t_kernel(tc, x, weight, bias, out):
             s_root, v_r = front(a, b)
             v_mid, v_den, s_q, v_end = back(a, b)
             root[e] = [s_root]
-            half1[e + 1] = v_r + half1.get(e + 1, [])
-            gate[e + 2] = powers(a)
-            gate[e + 3] = powers(a + POW_COLS)
-            half1[e + 4] = half1.get(e + 4, []) + v_mid + v_den
-            first_s[e + 5] = [s_q]
-            half1[e + 5] = half1.get(e + 5, []) + v_end
+            half2[e] = v_r
+            gate[e + 1] = powers(a, b)
+            half1[e + 2] = v_mid + v_den
+            first_s[e + 3] = [s_q]
+            half1[e + 3] = v_end
 
         make_identity(nc, ident[:])
         v.memset(half[:], 0.5)
@@ -386,7 +387,6 @@ def tile_hypequalizedlinear_t_kernel(tc, x, weight, bias, out):
         early_s[2] = [act(junk_d[1][:], b_pos[:], ACT.Square, y2[:])]
         half2[3] = [ts(y2p1[:], y2[:], 1.0, None, ALU.add)]
 
-        dots = []
         for s in range(NCH):
             fin = s >= LAG
             if s % 2 == 0 and s // 2 + LOOKAHEAD < NCH // 2:
@@ -400,9 +400,9 @@ def tile_hypequalizedlinear_t_kernel(tc, x, weight, bias, out):
                 gate[s][1]()
             for f in first_s.get(s, []):
                 f()
-            first = copies(s, (G_ON_S if s in gate else N_ON_S) if fin else 0)
-            squares, v_squares = x_squares(s, 1 if s in (1, 3, 5) else 0)
-            for f in squares[:1] + early_s.get(s, []):
+            first = copies(s, (0 if s in gate else 2) if fin else 0)
+            squares, v_squares = x_squares(s, 1 if s in XV else 0)
+            for f in (m_squares(s - 2) if s >= 2 else []) + root.get(s, []) + squares[:1] + early_s.get(s, []) + squares[1:]:
                 f()
             if s in first_v:
                 for f in first + first_v[s]:
@@ -413,82 +413,60 @@ def tile_hypequalizedlinear_t_kernel(tc, x, weight, bias, out):
                 calls, relus = finish(s - LAG)
                 first += calls
             if s >= 3:
-                dots += m_dot_b(s - 3)
-            n_dots = (6 if s in gate else max(2, len(dots) - 4)) if s > 4 else len(dots)
-            first += dots[:n_dots]
-            dots = dots[n_dots:]
+                first += m_dot_b(s - 3)
             weave(first, half1.get(s, []))
             if s + 1 < NCH:
                 transposes(s + 1)
-
-            sums = m_squares(s - 2) if s >= 2 else []
-            for f in squares[1:3] + sums + root.get(s, []) + squares[3:]:
-                f()
             terms = bias_terms(s + 1 - LAG, False) if s + 1 >= LAG else []
             weave(relus + v_squares + terms, half2.get(s, []))
             if s + 1 >= LAG:
                 products(s + 1 - LAG, ps_m2, "m2", m2_of)
 
-        last = NT - GROUP
-        mid_p, den_p, q_p, end_p = back(last - GROUP, last)
-        mid_l, den_l, q_l, end_l = back(last, NT)
-        root_a, r_a = front(last, last + POW_COLS)
-        root_b, r_b = front(last + POW_COLS, NT)
-        base_p, power_p = gate[NCH]
-        base_a, power_a = powers(last)
-        base_b, power_b = powers(last + POW_COLS)
-        c0 = NCH - LAG
-        c_p = c0 + 3
-        c_l = c_p + 4
-
-        def do(*calls):
+        def do(calls):
             for f in calls:
                 f()
 
-        base_p()
+        last = NT - GROUP
+        end_p = half1[NCH]
+        mid_l, den_l, q_l, end_l = back(last, NT)
+        root_l, r_l = front(last, NT)
+        base_l, power_l = powers(last, NT)
+        c0 = NCH - LAG
+        c_l = last // CH
+
+        do(first_s[NCH])
         quantise(NCH - 1)
         products(NCH - 1, ps_mm, "mm", mm_of)
-        power_p()
         products(c0 + 1, ps_m2, "m2", m2_of)
-        do(*m_squares(NCH - 2), root_a)
-        do(*bias_terms(c0 + 1, True), *m_squares(NCH - 1), root_b)
-        do(*bias_terms(c0 + 2, True))
+        products(c0 + 2, ps_xt, "xt", m2_of)
+        products(c0 + 3, ps_xt, "xt", m2_of)
+        do(m_squares(NCH - 2) + m_squares(NCH - 1) + [root_l])
         y0, relu0 = finish(c0)
-        y1, relu1 = finish(c0 + 1)
-        do(*dots, *y0, *m_dot_b(NCH - 3), *y1, *m_dot_b(NCH - 2))
-        products(c0 + 2, ps_m2, "m2", m2_of)
-        products(c_p, ps_xt, "xt", m2_of)
-        products(c_p + 1, ps_xt, "xt", m2_of)
-        y2_, relu2 = finish(c0 + 2)
-        weave(relu0 + relu1 + y2_, r_a + mid_p + den_p)
-        q_p()
-        weave(relu2, end_p)
-        base_a()
-        power_a()
-        for c in range(c_p, c_l):
-            do(*bias_terms(c, True))
-        do(*m_dot_b(NCH - 1))
-        products(c_p + 2, ps_m2, "m2", m2_of)
-        products(c_p + 3, ps_m2, "m2", m2_of)
-        y3, relu3 = finish(c_p)
-        y4, relu4 = finish(c_p + 1)
-        do(*y3, *y4)
-        weave(relu3 + relu4, r_b)
-        base_b()
-        power_b()
-        y5, relu5 = finish(c_p + 2)
-        y6, relu6 = finish(c_p + 3)
-        do(*y5, *y6)
-        for c in range(c_l, c_l + 2):
-            products(c, ps_xt, "xt", m2_of)
-        for c in range(c_l + 2, NCH):
-            products(c, ps_m2, "m2", m2_of)
-        weave(relu5, mid_l + den_l)
+        weave(y0 + m_dot_b(NCH - 3) + m_dot_b(NCH - 2), end_p)
+        for c in range(c0 + 1, c_l):
+            do(bias_terms(c, True))
+        products(c0 + 4, ps_m2, "m2", m2_of)
+        weave(relu0 + m_dot_b(NCH - 1), r_l)
+        base_l()
+        power_l()
+        relus = []
+        for c in range(c0 + 1, c0 + 4):
+            yc, rc = finish(c)
+            do(yc)
+            relus += rc
+        products(c_l, ps_m2, "m2", m2_of)
+        products(c_l + 1, ps_xt, "xt", m2_of)
+        products(c_l + 2, ps_xt, "xt", m2_of)
+        yc, rc = finish(c0 + 4)
+        weave(relus + yc, mid_l + den_l)
         q_l()
-        weave(relu6, end_l)
-        do(*bias_terms(c_l, False))
+        products(c_l + 3, ps_m2, "m2", m2_of)
+        weave(rc, end_l)
         for c in range(c_l + 1, NCH):
-            do(*bias_terms(c, True))
-        for c in range(c_l, NCH):
-            yc, reluc = finish(c)
-            do(*yc, *reluc)
+            do(scaled_products(c))
+        do(bias_terms(c_l, False))
+        yc, rc = finish(c_l)
+        do(yc + rc)
+        for c in range(c_l + 1, NCH):
+            yc, rc = finish(c, True)
+            do(yc + rc)

@@ -1,3 +1,4 @@
+import math
 from contextlib import ExitStack
 
 import concourse.mybir as mybir
@@ -21,7 +22,8 @@ CH = 4
 NCH = NT // CH
 GROUP = 16
 LAG = 9
-XV = (1, 3, 5)
+XV = (1, 3)
+GRAMS = 12
 LOOKAHEAD = 4
 
 
@@ -36,7 +38,8 @@ def tile_hypequalizedlinear_t_kernel(tc, x, weight, bias, out):
         bpool = ctx.enter_context(tc.tile_pool(name="bpool", bufs=4))
         ypool = ctx.enter_context(tc.tile_pool(name="ypool", bufs=4))
         ps_xt = ctx.enter_context(tc.psum_pool(name="ps_xt", bufs=2))
-        ps_mm = ctx.enter_context(tc.psum_pool(name="ps_mm", bufs=4))
+        ps_mm = ctx.enter_context(tc.psum_pool(name="ps_mm", bufs=3))
+        ps_g = ctx.enter_context(tc.psum_pool(name="ps_g", bufs=1))
         ps_m2 = ctx.enter_context(tc.psum_pool(name="ps_m2", bufs=2))
 
         ctx.enter_context(tc.manual_schedule())
@@ -64,11 +67,17 @@ def tile_hypequalizedlinear_t_kernel(tc, x, weight, bias, out):
         w_codes = const.tile([P, DOUT], U32, name="w_codes", align_bytes=64)
         w_scales = const.tile([P, DOUT], U8, name="w_scales", align_bytes=64)
         u_f = const.tile([P, DOUT], F32, name="u_f")
+        junk_g = const.tile([P, P], F32, name="junk_g")
+        gram_bank = ps_g.tile([P, P], F32, name="gram_bank")
         b_pos = const.tile([P, DOUT], F32, name="b_pos")
         b_neg = const.tile([P, DOUT], F32, name="b_neg")
         un2 = col("un2")
         un2c = col("un2c")
         un = col("un")
+        e_sq = col("e_sq")
+        eu = col("eu")
+        eu1 = col("eu1")
+        reu = col("reu")
         th = col("th")
         run = col("run")
         kk = col("kk")
@@ -203,6 +212,15 @@ def tile_hypequalizedlinear_t_kernel(tc, x, weight, bias, out):
                     v_calls.append(stt(junk_v[j][:], xt_, 1.0, xt_, ALU.mult, ALU.mult, acc))
             return calls, v_calls
 
+        def gram(c):
+            for i in range(4):
+                rows_i = g_of[c][:, (CH - 1) * K + i : CH * K : 4]
+                nc.tensor.matmul(gram_bank[:], lhsT=rows_i, rhs=rows_i, start=i == 0, stop=i == 3)
+
+        def diagonal(c):
+            t = c * CH + CH - 1
+            return stt(junk_g[:], gram_bank[:], 1.0, ident[:], ALU.mult, ALU.mult, s2[:, 0, t : t + 1])
+
         def quantise(c):
             t0 = c * CH
             v.quantize_mx(
@@ -237,10 +255,11 @@ def tile_hypequalizedlinear_t_kernel(tc, x, weight, bias, out):
                 for j in range(CH)
             ]
 
-        def store(c):
+        def store(c, n):
+            hi = (c % 2 + 1) * CH * DOUT
             return lambda: nc.sync.dma_start(
-                out=ov[:, (c - 1) * CH : (c + 1) * CH, :],
-                in_=y_of[c // 2][:].rearrange("p (t o) -> p t o", o=DOUT),
+                out=ov[:, (c + 1 - n) * CH : (c + 1) * CH, :],
+                in_=y_of[c // 2][:, hi - n * CH * DOUT : hi].rearrange("p (t o) -> p t o", o=DOUT),
             )
 
         def bias_terms(c, on_scalar):
@@ -280,8 +299,10 @@ def tile_hypequalizedlinear_t_kernel(tc, x, weight, bias, out):
                     calls.append(stt(ysl, m2_of[c][:, j * P : (j + 1) * P], al[:, t : t + 1], term, ALU.mult, ALU.add))
             ysl = y[:, off : off + CH * DOUT]
             last = [stt(ysl, ysl, 0.2, ysl, ALU.mult, ALU.max)]
-            if c % 2 == 1:
-                last.append(store(c))
+            if c >= NCH - 4:
+                last.append(store(c, 1))
+            elif c % 2 == 1:
+                last.append(store(c, 2))
             return calls, last
 
         def powers(a, b):
@@ -351,6 +372,7 @@ def tile_hypequalizedlinear_t_kernel(tc, x, weight, bias, out):
 
         make_identity(nc, ident[:])
         v.memset(half[:], 0.5)
+        v.tensor_scalar(out=e_sq[:], in0=half[:], scalar1=0.0, scalar2=math.e * math.e, op0=ALU.mult, op1=ALU.add)
         sc.dma_start(out=bias_bc[:], in_=bias.partition_broadcast(P))
         load(0, 4)
         nc.sync.dma_start(out=w_raw[:], in_=weight)
@@ -367,6 +389,7 @@ def tile_hypequalizedlinear_t_kernel(tc, x, weight, bias, out):
             0: [
                 ts(un2c[:], un2[:], 1e-30, None, ALU.max),
                 gtt(un[:], un2c[:], half[:], ALU.pow),
+                gtt(eu[:], e_sq[:], un[:], ALU.pow),
                 ts(
                     w_grouped[:].rearrange("p (o u e) -> p o u e", u=2, e=2),
                     w_bank[:, 0 : 2 * P].bitcast(BF16).rearrange("p (u o e) -> p o u e", u=2, e=2),
@@ -378,8 +401,10 @@ def tile_hypequalizedlinear_t_kernel(tc, x, weight, bias, out):
                 rcp(run[:], un[:]),
             ]
         }
-        early_s[1] = [act(th[:], un[:], ACT.Tanh)]
         half2[1] = [
+            ts(eu1[:], eu[:], 1.0, None, ALU.add),
+            rcp(reu[:], eu1[:]),
+            ts(th[:], reu[:], -2.0, 1.0, ALU.mult, ALU.add),
             tt(kk[:], th[:], run[:], ALU.mult),
             ts(b_pos[:], u_f[:], kk[:], None, ALU.mult),
             ts(b_neg[:], u_f[:], kk[:], -1.0, ALU.mult, ALU.mult),
@@ -387,12 +412,15 @@ def tile_hypequalizedlinear_t_kernel(tc, x, weight, bias, out):
         early_s[2] = [act(junk_d[1][:], b_pos[:], ACT.Square, y2[:])]
         half2[3] = [ts(y2p1[:], y2[:], 1.0, None, ALU.add)]
 
+        grams = [s for s in range(LAG, NCH) if s not in gate][:GRAMS]
         for s in range(NCH):
             fin = s >= LAG
             if s % 2 == 0 and s // 2 + LOOKAHEAD < NCH // 2:
                 load(s // 2 + LOOKAHEAD, 1)
             if s in gate:
                 gate[s][0]()
+            if s - 1 in grams:
+                gram(s - 1)
             if s >= 1:
                 quantise(s - 1)
                 products(s - 1, ps_mm, "mm", mm_of)
@@ -400,9 +428,16 @@ def tile_hypequalizedlinear_t_kernel(tc, x, weight, bias, out):
                 gate[s][1]()
             for f in first_s.get(s, []):
                 f()
-            first = copies(s, (0 if s in gate else 2) if fin else 0)
+            sums = (m_squares(s - 2) if s >= 2 else []) + root.get(s, [])
+            if s in root:
+                for f in sums:
+                    f()
+                sums = []
+            first = copies(s, (2 if s not in gate else 1 if s <= grams[-1] else 0) if fin else 0)
             squares, v_squares = x_squares(s, 1 if s in XV else 0)
-            for f in (m_squares(s - 2) if s >= 2 else []) + root.get(s, []) + squares[:1] + early_s.get(s, []) + squares[1:]:
+            if s in grams:
+                squares = squares[: CH - 1]
+            for f in sums + squares[:1] + early_s.get(s, []) + squares[1:]:
                 f()
             if s in first_v:
                 for f in first + first_v[s]:
@@ -418,7 +453,8 @@ def tile_hypequalizedlinear_t_kernel(tc, x, weight, bias, out):
             if s + 1 < NCH:
                 transposes(s + 1)
             terms = bias_terms(s + 1 - LAG, False) if s + 1 >= LAG else []
-            weave(relus + v_squares + terms, half2.get(s, []))
+            diag = [diagonal(s - 1)] if s - 1 in grams else []
+            weave(relus + diag + v_squares + terms, half2.get(s, []))
             if s + 1 >= LAG:
                 products(s + 1 - LAG, ps_m2, "m2", m2_of)
 
@@ -458,7 +494,8 @@ def tile_hypequalizedlinear_t_kernel(tc, x, weight, bias, out):
         products(c_l + 1, ps_xt, "xt", m2_of)
         products(c_l + 2, ps_xt, "xt", m2_of)
         yc, rc = finish(c0 + 4)
-        weave(relus + yc, mid_l + den_l)
+        do(relus[:1])
+        weave(relus[1:] + yc, mid_l + den_l)
         q_l()
         products(c_l + 3, ps_m2, "m2", m2_of)
         weave(rc, end_l)
@@ -466,7 +503,9 @@ def tile_hypequalizedlinear_t_kernel(tc, x, weight, bias, out):
             do(scaled_products(c))
         do(bias_terms(c_l, False))
         yc, rc = finish(c_l)
-        do(yc + rc)
+        do(yc)
         for c in range(c_l + 1, NCH):
-            yc, rc = finish(c, True)
+            yc, r_next = finish(c, True)
             do(yc + rc)
+            rc = r_next
+        do(rc)

import math
from contextlib import ExitStack

import concourse.mybir as mybir
from concourse.masks import make_identity

FLOPS = 2 * 16384 * 512 * 128

F32 = mybir.dt.float32
BF16 = mybir.dt.bfloat16
U32 = mybir.dt.uint32
U8 = mybir.dt.uint8
FP8X4 = mybir.dt.float8_e4m3fn_x4
ALU = mybir.AluOpType
ACT = mybir.ActivationFunctionType

P = 128
K = 512
DOUT = 128
NT = 128
CH = 4
NCH = NT // CH
GROUP = 16
LAG = 9
XV = (1, 3)
GRAMS = 12
LOOKAHEAD = 4


def tile_hypequalizedlinear_t_kernel(tc, x, weight, bias, out):
    nc = tc.nc
    xv = x.rearrange("(p t) k -> p t k", t=NT)
    ov = out.rearrange("(p t) o -> p t o", t=NT)
    with ExitStack() as ctx:
        const = ctx.enter_context(tc.tile_pool(name="const", bufs=1))
        xpool = ctx.enter_context(tc.tile_pool(name="xpool", bufs=6))
        gpool = ctx.enter_context(tc.tile_pool(name="gpool", bufs=3))
        bpool = ctx.enter_context(tc.tile_pool(name="bpool", bufs=4))
        ypool = ctx.enter_context(tc.tile_pool(name="ypool", bufs=4))
        ps_xt = ctx.enter_context(tc.psum_pool(name="ps_xt", bufs=2))
        ps_mm = ctx.enter_context(tc.psum_pool(name="ps_mm", bufs=3))
        ps_g = ctx.enter_context(tc.psum_pool(name="ps_g", bufs=1))
        ps_m2 = ctx.enter_context(tc.psum_pool(name="ps_m2", bufs=2))

        ctx.enter_context(tc.manual_schedule())
        v = nc.vector
        sc = nc.scalar
        g_ = nc.gpsimd

        def col(name):
            return const.tile([P, 1], F32, name=name)

        def wide(name, n=1):
            if n == 1:
                return const.tile([P, NT], F32, name=name)
            return const.tile([P, n, NT], F32, name=name)

        ident = const.tile([P, P], F32, name="ident")
        half = col("half")
        w_raw = const.tile([P, K], BF16, name="w_raw")
        bias_bc = const.tile([P, DOUT], BF16, name="bias_bc")
        junk_c = [const.tile([P, K], BF16, name="junk_c%d" % i) for i in range(4)]
        junk_v = [const.tile([P, K], BF16, name="junk_v%d" % i) for i in range(4)]
        junk_d = [const.tile([P, DOUT], F32, name="junk_d%d" % i) for i in range(4)]
        junk_e = [const.tile([P, DOUT], F32, name="junk_e%d" % i) for i in range(4)]
        w_grouped = const.tile([P, K], BF16, name="w_grouped", align_bytes=64)
        w_codes = const.tile([P, DOUT], U32, name="w_codes", align_bytes=64)
        w_scales = const.tile([P, DOUT], U8, name="w_scales", align_bytes=64)
        u_f = const.tile([P, DOUT], F32, name="u_f")
        junk_g = const.tile([P, P], F32, name="junk_g")
        gram_bank = ps_g.tile([P, P], F32, name="gram_bank")
        b_pos = const.tile([P, DOUT], F32, name="b_pos")
        b_neg = const.tile([P, DOUT], F32, name="b_neg")
        un2 = col("un2")
        un2c = col("un2c")
        un = col("un")
        e_sq = col("e_sq")
        eu = col("eu")
        eu1 = col("eu1")
        reu = col("reu")
        th = col("th")
        run = col("run")
        kk = col("kk")
        y2 = col("y2")
        y2p1 = col("y2p1")
        codes = const.tile([P, NT * P], U32, name="codes", align_bytes=64)
        scales = const.tile([P, NT * P], U8, name="scales", align_bytes=64)
        s2 = wide("s2", 2)
        pb = wide("pb")
        al = wide("al")
        c_nrm = wide("c_nrm", 3)
        c_rnrm = wide("c_rnrm", 3)
        c_base = wide("c_base")
        c_r = wide("c_r")
        c_e = wide("c_e")
        c_e1 = wide("c_e1")
        c_re = wide("c_re")
        c_t = wide("c_t")
        c_s = wide("c_s")
        c_x2 = wide("c_x2")
        nbe = wide("nbe")
        c_xy = wide("c_xy")
        c_d0 = wide("c_d0")
        c_den = wide("c_den")
        c_num = wide("c_num")
        c_nd = wide("c_nd")
        c_q = wide("c_q")
        c_mx = wide("c_mx")
        c_rf = wide("c_rf")
        c_as = wide("c_as")

        xs_of = {}
        xt_of = {}
        g_of = {}
        mm_of = {}
        m2_of = {}
        bb_of = {}
        y_of = {}

        def ts(o, i, s1, s2_, o0, o1=None):
            if o1 is None:
                return lambda: v.tensor_scalar(out=o, in0=i, scalar1=s1, scalar2=None, op0=o0)
            return lambda: v.tensor_scalar(out=o, in0=i, scalar1=s1, scalar2=s2_, op0=o0, op1=o1)

        def tt(o, i0, i1, op):
            return lambda: v.tensor_tensor(out=o, in0=i0, in1=i1, op=op)

        def stt(o, i0, s, i1, o0, o1, acc=None):
            return lambda: v.scalar_tensor_tensor(out=o, in0=i0, scalar=s, in1=i1, op0=o0, op1=o1, accum_out=acc)

        def rcp(o, i):
            return lambda: v.reciprocal(out=o, in_=i)

        def act(o, i, func, acc=None, add=0.0):
            return lambda: sc.activation(out=o, in_=i, func=func, bias=add, accum_out=acc)

        def scaled(o, i, s):
            return lambda: sc.activation(out=o, in_=i, func=ACT.Copy, scale=s)

        def gtt(o, i0, i1, op):
            return lambda: g_.tensor_tensor(out=o, in0=i0, in1=i1, op=op)

        def weave(bulk, extras):
            done = 0
            for n, f in enumerate(bulk):
                f()
                while done < len(extras) and (done + 1) * len(bulk) <= (n + 1) * len(extras):
                    extras[done]()
                    done += 1
            for f in extras[done:]:
                f()

        def mx(dst, t):
            nc.tensor.matmul_mx(
                out=dst,
                lhsT=codes[:, t * P : (t + 1) * P].bitcast(FP8X4),
                lhsT_scale=scales[:, t * P : (t + 1) * P],
                rhs=w_codes[:].bitcast(FP8X4),
                rhs_scale=w_scales[:],
                start=True,
                stop=True,
            )

        def load(blk, parts):
            xs = xpool.tile([P, 2 * CH * K], BF16, name="xs")
            xs_of[blk] = xs
            n = 2 * CH // parts
            for i in range(parts):
                nc.sync.dma_start(
                    out=xs[:, i * n * K : (i + 1) * n * K].rearrange("p (t k) -> p t k", k=K),
                    in_=xv[:, blk * 2 * CH + i * n : blk * 2 * CH + (i + 1) * n, :],
                )

        def transposes(c):
            xw = xs_of[c // 2][:].bitcast(F32)
            banks = []
            for h in range(2):
                xt = ps_xt.tile([P, 512], F32, name="xt")
                banks.append(xt)
                for q in range(4):
                    loc = (c % 2) * CH + 2 * h + q // 2
                    w0 = loc * (K // 2)
                    nc.tensor.transpose(xt[:, q * P : (q + 1) * P], xw[:, w0 + q % 2 : w0 + K // 2 : 2], ident[:])
            xt_of[c] = banks

        def copies(c, on_scalar):
            g = gpool.tile([P, CH * K], BF16, name="g", align_bytes=64)
            g_of[c] = g
            gw = g[:].bitcast(F32)
            calls = []
            for h in range(2):
                dst = gw[:, h * 512 : (h + 1) * 512].rearrange("p (t r u) -> p t r u", t=2, u=2)
                src = xt_of[c][h][:].rearrange("p (t u r) -> p t r u", t=2, u=2)
                if h >= 2 - on_scalar:
                    sc.copy(out=dst, in_=src)
                else:
                    calls.append(lambda dst=dst, src=src: v.tensor_copy(out=dst, in_=src))
            return calls

        def x_squares(c, n_v):
            xs = xs_of[c // 2]
            calls = []
            v_calls = []
            for j in range(CH):
                loc = (c % 2) * CH + j
                t = c * CH + j
                xt_ = xs[:, loc * K : (loc + 1) * K]
                acc = s2[:, 0, t : t + 1]
                if j < CH - n_v:
                    calls.append(act(junk_c[j][:], xt_, ACT.Square, acc))
                else:
                    v_calls.append(stt(junk_v[j][:], xt_, 1.0, xt_, ALU.mult, ALU.mult, acc))
            return calls, v_calls

        def gram(c):
            for i in range(4):
                rows_i = g_of[c][:, (CH - 1) * K + i : CH * K : 4]
                nc.tensor.matmul(gram_bank[:], lhsT=rows_i, rhs=rows_i, start=i == 0, stop=i == 3)

        def diagonal(c):
            t = c * CH + CH - 1
            return stt(junk_g[:], gram_bank[:], 1.0, ident[:], ALU.mult, ALU.mult, s2[:, 0, t : t + 1])

        def quantise(c):
            t0 = c * CH
            v.quantize_mx(
                out=codes[:, t0 * P : (t0 + CH) * P].bitcast(FP8X4),
                scales=scales[:, t0 * P : (t0 + CH) * P],
                in_=g_of[c][:],
            )

        def products(c, pool, name, keep):
            bank = pool.tile([P, 512], F32, name=name)
            keep[c] = bank
            for j in range(CH):
                mx(bank[:, j * P : (j + 1) * P], c * CH + j)

        def m_squares(c):
            return [
                act(junk_d[j][:], mm_of[c][:, j * P : (j + 1) * P], ACT.Square, s2[:, 1, c * CH + j : c * CH + j + 1])
                for j in range(CH)
            ]

        def m_dot_b(c):
            return [
                stt(
                    junk_e[j][:],
                    mm_of[c][:, j * P : (j + 1) * P],
                    2.0,
                    b_pos[:],
                    ALU.mult,
                    ALU.mult,
                    pb[:, c * CH + j : c * CH + j + 1],
                )
                for j in range(CH)
            ]

        def store(c, n):
            hi = (c % 2 + 1) * CH * DOUT
            return lambda: nc.sync.dma_start(
                out=ov[:, (c + 1 - n) * CH : (c + 1) * CH, :],
                in_=y_of[c // 2][:, hi - n * CH * DOUT : hi].rearrange("p (t o) -> p t o", o=DOUT),
            )

        def bias_terms(c, on_scalar):
            bb = bpool.tile([P, CH * DOUT], F32, name="bb")
            bb_of[c] = bb
            calls = []
            for j in range(CH):
                t = c * CH + j
                dst = bb[:, j * P : (j + 1) * P]
                if on_scalar:
                    calls.append(scaled(dst, b_neg[:], nbe[:, t : t + 1]))
                else:
                    calls.append(ts(dst, b_neg[:], nbe[:, t : t + 1], None, ALU.mult))
            return calls

        def scaled_products(c):
            bb = bpool.tile([P, CH * DOUT], F32, name="bb")
            bb_of[c] = bb
            return [
                scaled(bb[:, j * P : (j + 1) * P], m2_of[c][:, j * P : (j + 1) * P], al[:, c * CH + j : c * CH + j + 1])
                for j in range(CH)
            ]

        def finish(c, is_scaled=False):
            if c % 2 == 0:
                y_of[c // 2] = ypool.tile([P, 2 * CH * DOUT], F32, name="y")
            y = y_of[c // 2]
            off = (c % 2) * CH * DOUT
            calls = []
            for j in range(CH):
                t = c * CH + j
                ysl = y[:, off + j * P : off + (j + 1) * P]
                term = bb_of[c][:, j * P : (j + 1) * P]
                if is_scaled:
                    calls.append(stt(ysl, b_neg[:], nbe[:, t : t + 1], term, ALU.mult, ALU.add))
                else:
                    calls.append(stt(ysl, m2_of[c][:, j * P : (j + 1) * P], al[:, t : t + 1], term, ALU.mult, ALU.add))
            ysl = y[:, off : off + CH * DOUT]
            last = [stt(ysl, ysl, 0.2, ysl, ALU.mult, ALU.max)]
            if c >= NCH - 4:
                last.append(store(c, 1))
            elif c % 2 == 1:
                last.append(store(c, 2))
            return calls, last

        def powers(a, b):
            sl = slice(a, b)
            return (
                ts(c_base[:, sl], c_rnrm[:, 2, sl], -2.0, -1.0, ALU.mult, ALU.add),
                gtt(c_e[:, sl], c_base[:, sl], c_r[:, sl], ALU.pow),
            )

        def front(a, b):
            sl = slice(a, b)
            s_root = act(c_nrm[:, 0:2, sl], s2[:, :, sl], ACT.Sqrt, add=1e-30)
            v_r = [
                ts(c_nrm[:, 2, sl], c_nrm[:, 0, sl], 1.0 - 1e-5, 1.0, ALU.min, ALU.subtract),
                rcp(c_rnrm[:, :, sl], c_nrm[:, :, sl]),
                tt(c_r[:, sl], c_nrm[:, 1, sl], c_rnrm[:, 0, sl], ALU.mult),
            ]
            return s_root, v_r

        def back(a, b):
            sl = slice(a, b)
            v_mid = [
                ts(c_e1[:, sl], c_e[:, sl], 1.0, None, ALU.add),
                rcp(c_re[:, sl], c_e1[:, sl]),
                ts(c_t[:, sl], c_re[:, sl], -2.0, 1.0, ALU.mult, ALU.add),
                tt(c_s[:, sl], c_t[:, sl], c_rnrm[:, 1, sl], ALU.mult),
                tt(c_x2[:, sl], c_t[:, sl], c_t[:, sl], ALU.mult),
                tt(c_xy[:, sl], c_s[:, sl], pb[:, sl], ALU.mult),
            ]
            v_den = [
                stt(c_d0[:, sl], c_x2[:, sl], y2[:], c_xy[:, sl], ALU.mult, ALU.add),
                stt(c_num[:, sl], c_x2[:, sl], y2[:], c_xy[:, sl], ALU.add, ALU.add),
                ts(c_den[:, sl], c_d0[:, sl], 1.0, 1e-15, ALU.add, ALU.max),
                stt(c_as[:, sl], c_xy[:, sl], y2p1[:], c_s[:, sl], ALU.add, ALU.mult),
                stt(c_nd[:, sl], c_num[:, sl], 0.0, c_den[:, sl], ALU.max, ALU.mult),
            ]

            def s_q():
                sc.activation(out=c_q[:, sl], in_=c_nd[:, sl], func=ACT.Sqrt, scale=1.0 / (0.999 * 0.999))

            v_end = [
                tt(c_mx[:, sl], c_den[:, sl], c_q[:, sl], ALU.max),
                rcp(c_rf[:, sl], c_mx[:, sl]),
                stt(nbe[:, sl], c_x2[:, sl], 1.0, c_rf[:, sl], ALU.subtract, ALU.mult),
                tt(al[:, sl], c_as[:, sl], c_rf[:, sl], ALU.mult),
            ]
            return v_mid, v_den, s_q, v_end

        half1 = {}
        half2 = {}
        gate = {}
        root = {}
        first_s = {}
        early_s = {}

        for b in range(GROUP, NT, GROUP):
            a = b - GROUP
            e = b // CH + 1
            s_root, v_r = front(a, b)
            v_mid, v_den, s_q, v_end = back(a, b)
            root[e] = [s_root]
            half2[e] = v_r
            gate[e + 1] = powers(a, b)
            half1[e + 2] = v_mid + v_den
            first_s[e + 3] = [s_q]
            half1[e + 3] = v_end

        make_identity(nc, ident[:])
        v.memset(half[:], 0.5)
        v.tensor_scalar(out=e_sq[:], in0=half[:], scalar1=0.0, scalar2=math.e * math.e, op0=ALU.mult, op1=ALU.add)
        sc.dma_start(out=bias_bc[:], in_=bias.partition_broadcast(P))
        load(0, 4)
        nc.sync.dma_start(out=w_raw[:], in_=weight)
        for blk in range(1, LOOKAHEAD):
            load(blk, 1)
        transposes(0)
        w_bank = ps_mm.tile([P, 512], F32, name="mm")
        w_words = w_raw[:].bitcast(F32)
        for u in range(2):
            nc.tensor.transpose(w_bank[:, u * P : (u + 1) * P], w_words[:, u : K // 2 : 2], ident[:])
        v.tensor_scalar(out=u_f[:], in0=bias_bc[:], scalar1=0.1, scalar2=None, op0=ALU.mult)
        sc.activation(out=junk_d[0][:], in_=u_f[:], func=ACT.Square, accum_out=un2[:])
        first_v = {
            0: [
                ts(un2c[:], un2[:], 1e-30, None, ALU.max),
                gtt(un[:], un2c[:], half[:], ALU.pow),
                gtt(eu[:], e_sq[:], un[:], ALU.pow),
                ts(
                    w_grouped[:].rearrange("p (o u e) -> p o u e", u=2, e=2),
                    w_bank[:, 0 : 2 * P].bitcast(BF16).rearrange("p (u o e) -> p o u e", u=2, e=2),
                    0.1,
                    None,
                    ALU.mult,
                ),
                lambda: v.quantize_mx(out=w_codes[:].bitcast(FP8X4), scales=w_scales[:], in_=w_grouped[:]),
                rcp(run[:], un[:]),
            ]
        }
        half2[1] = [
            ts(eu1[:], eu[:], 1.0, None, ALU.add),
            rcp(reu[:], eu1[:]),
            ts(th[:], reu[:], -2.0, 1.0, ALU.mult, ALU.add),
            tt(kk[:], th[:], run[:], ALU.mult),
            ts(b_pos[:], u_f[:], kk[:], None, ALU.mult),
            ts(b_neg[:], u_f[:], kk[:], -1.0, ALU.mult, ALU.mult),
        ]
        early_s[2] = [act(junk_d[1][:], b_pos[:], ACT.Square, y2[:])]
        half2[3] = [ts(y2p1[:], y2[:], 1.0, None, ALU.add)]

        grams = [s for s in range(LAG, NCH) if s not in gate][:GRAMS]
        for s in range(NCH):
            fin = s >= LAG
            if s % 2 == 0 and s // 2 + LOOKAHEAD < NCH // 2:
                load(s // 2 + LOOKAHEAD, 1)
            if s in gate:
                gate[s][0]()
            if s - 1 in grams:
                gram(s - 1)
            if s >= 1:
                quantise(s - 1)
                products(s - 1, ps_mm, "mm", mm_of)
            if s in gate:
                gate[s][1]()
            for f in first_s.get(s, []):
                f()
            sums = (m_squares(s - 2) if s >= 2 else []) + root.get(s, [])
            if s in root:
                for f in sums:
                    f()
                sums = []
            first = copies(s, (2 if s not in gate else 1 if s <= grams[-1] else 0) if fin else 0)
            squares, v_squares = x_squares(s, 1 if s in XV else 0)
            if s in grams:
                squares = squares[: CH - 1]
            for f in sums + squares[:1] + early_s.get(s, []) + squares[1:]:
                f()
            if s in first_v:
                for f in first + first_v[s]:
                    f()
                first = []
            relus = []
            if fin:
                calls, relus = finish(s - LAG)
                first += calls
            if s >= 3:
                first += m_dot_b(s - 3)
            weave(first, half1.get(s, []))
            if s + 1 < NCH:
                transposes(s + 1)
            terms = bias_terms(s + 1 - LAG, False) if s + 1 >= LAG else []
            diag = [diagonal(s - 1)] if s - 1 in grams else []
            weave(relus + diag + v_squares + terms, half2.get(s, []))
            if s + 1 >= LAG:
                products(s + 1 - LAG, ps_m2, "m2", m2_of)

        def do(calls):
            for f in calls:
                f()

        last = NT - GROUP
        end_p = half1[NCH]
        mid_l, den_l, q_l, end_l = back(last, NT)
        root_l, r_l = front(last, NT)
        base_l, power_l = powers(last, NT)
        c0 = NCH - LAG
        c_l = last // CH

        do(first_s[NCH])
        quantise(NCH - 1)
        products(NCH - 1, ps_mm, "mm", mm_of)
        products(c0 + 1, ps_m2, "m2", m2_of)
        products(c0 + 2, ps_xt, "xt", m2_of)
        products(c0 + 3, ps_xt, "xt", m2_of)
        do(m_squares(NCH - 2) + m_squares(NCH - 1) + [root_l])
        y0, relu0 = finish(c0)
        weave(y0 + m_dot_b(NCH - 3) + m_dot_b(NCH - 2), end_p)
        for c in range(c0 + 1, c_l):
            do(bias_terms(c, True))
        products(c0 + 4, ps_m2, "m2", m2_of)
        weave(relu0 + m_dot_b(NCH - 1), r_l)
        base_l()
        power_l()
        relus = []
        for c in range(c0 + 1, c0 + 4):
            yc, rc = finish(c)
            do(yc)
            relus += rc
        products(c_l, ps_m2, "m2", m2_of)
        products(c_l + 1, ps_xt, "xt", m2_of)
        products(c_l + 2, ps_xt, "xt", m2_of)
        yc, rc = finish(c0 + 4)
        do(relus[:1])
        weave(relus[1:] + yc, mid_l + den_l)
        q_l()
        products(c_l + 3, ps_m2, "m2", m2_of)
        weave(rc, end_l)
        for c in range(c_l + 1, NCH):
            do(scaled_products(c))
        do(bias_terms(c_l, False))
        yc, rc = finish(c_l)
        do(yc)
        for c in range(c_l + 1, NCH):
            yc, r_next = finish(c, True)
            do(yc + rc)
            rc = r_next
        do(rc)
